import numpy as np
import ml_dtypes


def mxq(x, axis, fmt="e4m3"):
    dtype, down = {"e4m3": (ml_dtypes.float8_e4m3fn, 7), "e5m2": (ml_dtypes.float8_e5m2, 14)}[fmt]
    v = np.moveaxis(np.asarray(x, np.float32).astype(ml_dtypes.bfloat16).astype(np.float64), axis, -1)
    blocks = v.reshape(v.shape[:-1] + (-1, 32))
    amax = np.abs(blocks).max(-1, keepdims=True)
    byte = np.maximum(np.where(amax > 0, np.frexp(amax)[1] - 1 + 127, 0) - down, 1)
    scale = np.exp2(byte - 127.0)
    codes = (blocks / scale).astype(np.float32).astype(dtype).astype(np.float64)
    return np.moveaxis((codes * scale).reshape(v.shape), -1, axis)


WIDE = False


def mx_kscale(k):
    if not WIDE:
        return np.ones(k)
    levels = np.array([10, -10, 5, -5, 0])
    a = np.random.permutation(np.resize(levels, k // 512 * 4)).reshape(k // 512, 4)
    idx = np.arange(k)
    return np.exp2(a[idx // 512, idx % 128 // 32])


BF16 = ml_dtypes.bfloat16


def bf(x):
    return np.asarray(x, np.float32).astype(BF16)


def f64(x):
    return np.asarray(x).astype(np.float64)


E2M1 = np.array([0.0, 0.5, 1.0, 1.5, 2.0, 3.0, 4.0, 6.0, -0.0, -0.5, -1.0, -1.5, -2.0, -3.0, -4.0, -6.0])


def pack_weight(w, fmt):
    k, n = w.shape
    w = f64(bf(w)).reshape(k // 32, 32, n)
    amax = np.abs(w).max(1)
    if fmt == "e4m3":
        byte = np.frexp(amax)[1] - 1 + 127 - 7
    else:
        mant, ex = np.frexp(amax / 6.0)
        byte = np.where(mant > 0.5, ex, ex - 1) + 127
    byte = np.clip(np.where(amax > 0, byte, 1), 1, 254)
    scaled = (w * np.exp2(127.0 - byte)[:, None, :]).reshape(k, n).astype(np.float32)
    by_word = np.ascontiguousarray(scaled.reshape(k // 512, 128, 4, n).transpose(0, 1, 3, 2))
    if fmt == "e4m3":
        words = by_word.astype(ml_dtypes.float8_e4m3fn).view(np.uint8)
    else:
        c = by_word.astype(ml_dtypes.float4_e2m1fn).view(np.uint8) & 0xF
        words = c[..., 0::2] | (c[..., 1::2] << 4)
    return np.ascontiguousarray(words), np.ascontiguousarray(byte.astype(np.uint8).reshape(k // 512, 16, n))


def unpack_weight(words, scales, fmt):
    g, p, n, _ = words.shape
    if fmt == "e4m3":
        vals = np.ascontiguousarray(words).view(ml_dtypes.float8_e4m3fn).astype(np.float64)
    else:
        nib = np.empty((g, p, n, 4), np.uint8)
        nib[..., 0::2] = words & 0xF
        nib[..., 1::2] = words >> 4
        vals = E2M1[nib]
    vals = vals * np.repeat(np.exp2(scales.astype(np.float64) - 127.0), 8, axis=1)[..., None]
    return vals.transpose(0, 1, 3, 2).reshape(g * 512, n)


B, S, D, N = 128, 32, 1024, 1024
EPS = 1e-5
FMT = "e4m3"


def batch_bn(x, g, b):
    m = x.mean(axis=0)
    v = x.var(axis=0)
    return g * (x - m) / np.sqrt(v + EPS) + b


def setup_inputs():
    t, u = mx_kscale(D), mx_kscale(D)
    s_z2 = bf(np.random.standard_normal((B, S, D)) * 0.6 + np.random.standard_normal(D) * 0.4)
    c_z2 = bf(np.random.standard_normal((B, D)) * 0.6 + np.random.standard_normal(D) * 0.4)
    s_g2 = bf((1.0 + 0.1 * np.random.standard_normal(D)) * t)
    s_be2 = bf(0.1 * np.random.standard_normal(D) * t)
    s_w3 = np.random.standard_normal((N, D)) * np.sqrt(2.0 / D) / t[None, :]
    s_w3_words, s_w3_scales = pack_weight(np.ascontiguousarray(s_w3.T), FMT)
    s_b3 = bf(0.1 * np.random.standard_normal(N))
    c_g2 = bf((1.0 + 0.1 * np.random.standard_normal(D)) * u)
    c_be2 = bf(0.1 * np.random.standard_normal(D) * u)
    c_w3 = np.random.standard_normal((N, D)) * np.sqrt(2.0 / D) / u[None, :]
    c_w3_words, c_w3_scales = pack_weight(np.ascontiguousarray(c_w3.T), FMT)
    c_b3 = bf(0.1 * np.random.standard_normal(N))
    return {"s_z2": s_z2,
            "c_z2": c_z2,
            "s_g2": s_g2,
            "s_be2": s_be2,
            "s_w3_words": s_w3_words,
            "s_w3_scales": s_w3_scales,
            "s_b3": s_b3,
            "c_g2": c_g2,
            "c_be2": c_be2,
            "c_w3_words": c_w3_words,
            "c_w3_scales": c_w3_scales,
            "c_b3": c_b3}


def reference(s_z2, c_z2, s_g2, s_be2, s_w3_words, s_w3_scales, s_b3, c_g2, c_be2, c_w3_words, c_w3_scales, c_b3):
    c_h = np.maximum(batch_bn(f64(c_z2), f64(c_g2), f64(c_be2)), 0.0)
    c_out = (mxq(c_h, 1, "e4m3") @ unpack_weight(c_w3_words, c_w3_scales, FMT)) + f64(c_b3)
    s_h = np.maximum(batch_bn(f64(s_z2), f64(s_g2), f64(s_be2)), 0.0)
    s_p = (mxq(s_h, 2, "e4m3") @ unpack_weight(s_w3_words, s_w3_scales, FMT)) + f64(s_b3)
    s_out = s_p * c_out[:, None, :]
    aggregated_c = s_out.max(axis=1)
    return (s_out, aggregated_c)

@@ -1,0 +1,235 @@
+from contextlib import ExitStack
+
+import concourse.mybir as mybir
+from concourse.masks import make_identity
+
+F32 = mybir.dt.float32
+BF16 = mybir.dt.bfloat16
+U8 = mybir.dt.uint8
+U32 = mybir.dt.uint32
+I32 = mybir.dt.int32
+FP8X4 = mybir.dt.float8_e4m3fn_x4
+ACT = mybir.ActivationFunctionType
+ALU = mybir.AluOpType
+
+P = 128
+B = 128
+SLICES = 32
+K = 1024
+N = 1024
+PACK = 4
+K_PASS = P * PACK
+PASSES = K // K_PASS
+PLANES = PASSES * PACK
+N_TILE = 512
+N_TILES = N // N_TILE
+LOAD = 4
+STORE = 2
+EPS = 1e-5
+
+FLOPS = 2 * (SLICES + 1) * B * K * N
+
+
+def tile_cgblock_pb_kernel(
+    tc,
+    s_z2,
+    c_z2,
+    s_g2,
+    s_be2,
+    s_w3_words,
+    s_w3_scales,
+    s_b3,
+    c_g2,
+    c_be2,
+    c_w3_words,
+    c_w3_scales,
+    c_b3,
+    out_0,
+    out_1,
+):
+    nc = tc.nc
+    with ExitStack() as pools:
+        keep = pools.enter_context(tc.tile_pool(name="keep", bufs=1))
+        small = pools.enter_context(tc.tile_pool(name="small", bufs=4))
+        work = pools.enter_context(tc.tile_pool(name="work", bufs=3))
+        stores = pools.enter_context(tc.tile_pool(name="stores", bufs=3))
+        psum_t = pools.enter_context(tc.psum_pool(name="psum_t", bufs=3))
+        psum_sum = pools.enter_context(tc.psum_pool(name="psum_sum", bufs=1))
+        psum_acc = pools.enter_context(tc.psum_pool(name="psum_acc", bufs=4))
+
+        ident = keep.tile([P, P], F32)
+        make_identity(nc, ident[:])
+        ones = keep.tile([P, 1], BF16)
+        nc.vector.memset(ones[:], 1.0)
+        eps = keep.tile([P, 1], F32)
+        nc.vector.memset(eps[:], EPS)
+
+        c_z = keep.tile([P, K], BF16)
+        nc.sync.dma_start(out=c_z[:], in_=c_z2)
+
+        w_planes = keep.tile([P, N], U8, align_bytes=64)
+        nc.vector.memset(w_planes[:].bitcast(I32), 0)
+        for quadrant in range(4):
+            for w, w_scales in enumerate((s_w3_scales, c_w3_scales)):
+                first = 32 * quadrant + 8 * w
+                nc.sync.dma_start(
+                    out=w_planes[first : first + 8, :].bitcast(I32),
+                    in_=w_scales[:, 4 * quadrant : 4 * quadrant + 4, :].bitcast(I32),
+                )
+
+        def load_words(words_dram, name):
+            words = keep.tile([P, PASSES, N], U32, name=name, align_bytes=64)
+            nc.sync.dma_start(
+                out=words[:].bitcast(I32),
+                in_=words_dram.rearrange("g p n t -> p g (n t)").bitcast(I32),
+            )
+            return words
+
+        def load_slices(first):
+            z = keep.tile([P, LOAD, K], BF16, name="z%d" % first)
+            nc.sync.dma_start(out=z[:], in_=s_z2[:, first : first + LOAD, :])
+            return z
+
+        c_words = load_words(c_w3_words, "c_words")
+        s_z = [load_slices(0)]
+        s_words = load_words(s_w3_words, "s_words")
+        for first in range(LOAD, SLICES, LOAD):
+            s_z.append(load_slices(first))
+
+        def load_by_feature(vector, name):
+            by_feature = keep.tile([P, PASSES, PACK], BF16, name=name)
+            with nc.allow_non_contiguous_dma(reason="2 KiB in runs of four neighbouring features"):
+                nc.scalar.dma_start(
+                    out=by_feature[:], in_=vector.rearrange("(g p t) -> p g t", g=PASSES, p=P, t=PACK)
+                )
+            return by_feature[:].rearrange("p g t -> p (g t)")
+
+        c_gain = load_by_feature(c_g2, "c_gain")
+        c_shift = load_by_feature(c_be2, "c_shift")
+        s_gain = load_by_feature(s_g2, "s_gain")
+        s_shift = load_by_feature(s_be2, "s_shift")
+
+        c_bias = keep.tile([P, N], BF16)
+        nc.scalar.dma_start(out=c_bias[:], in_=c_b3.partition_broadcast(P))
+        s_bias = keep.tile([P, N], BF16)
+        nc.scalar.dma_start(out=s_bias[:], in_=s_b3.partition_broadcast(P))
+
+        sums = psum_sum.tile([P, (SLICES + 1) * PLANES], F32)
+
+        def hidden_layer(unit, z_unit, gain, shift):
+            z_t = psum_t.tile([P, PASSES * 2, B], F32)
+            z_words = z_unit.bitcast(F32)
+            for g in range(PASSES):
+                for h in range(2):
+                    nc.tensor.transpose(
+                        z_t[:, 2 * g + h, :], z_words[:, 256 * g + h : 256 * (g + 1) : 2], ident[:]
+                    )
+            unit_sums = sums[:, unit * PLANES : (unit + 1) * PLANES]
+            for g in range(PASSES):
+                for t in range(PACK):
+                    nc.tensor.matmul(
+                        unit_sums[:, PACK * g + t : PACK * g + t + 1],
+                        lhsT=z_unit[:, K_PASS * g + t : K_PASS * (g + 1) : PACK],
+                        rhs=ones[:],
+                        start=True,
+                        stop=True,
+                    )
+            halves = z_t[:].bitcast(BF16).rearrange("p q (b e) -> p q e b", e=2)
+
+            def plane(f):
+                return halves[:, f // 2, f % 2, :]
+
+            neg_mean = small.tile([P, PLANES], F32)
+            nc.scalar.mul(out=neg_mean[:], in_=unit_sums, mul=-1.0 / B)
+            squares = work.tile([P, PLANES, B], BF16)
+            sum_sq = small.tile([P, PLANES], F32)
+            for f in range(PLANES):
+                nc.scalar.activation(
+                    out=squares[:, f, :],
+                    in_=plane(f),
+                    func=ACT.Square,
+                    bias=neg_mean[:, f : f + 1],
+                    scale=1.0,
+                    accum_out=sum_sq[:, f : f + 1],
+                )
+            std = small.tile([P, PLANES], F32)
+            nc.scalar.activation(out=std[:], in_=sum_sq[:], func=ACT.Sqrt, bias=eps[:], scale=1.0 / B)
+            rstd = small.tile([P, PLANES], F32)
+            nc.vector.reciprocal(out=rstd[:], in_=std[:])
+            slope = small.tile([P, PLANES], F32)
+            nc.gpsimd.tensor_tensor(out=slope[:], in0=rstd[:], in1=gain, op=ALU.mult)
+            centre = small.tile([P, PLANES], F32)
+            nc.gpsimd.tensor_tensor(out=centre[:], in0=slope[:], in1=neg_mean[:], op=ALU.mult)
+            offset = small.tile([P, PLANES], F32)
+            nc.gpsimd.tensor_tensor(out=offset[:], in0=centre[:], in1=shift, op=ALU.add)
+
+            h_planes = work.tile([P, PLANES, B], BF16)
+            for f in range(PLANES):
+                nc.scalar.activation(
+                    out=h_planes[:, f, :],
+                    in_=plane(f),
+                    func=ACT.Relu,
+                    bias=offset[:, f : f + 1],
+                    scale=slope[:, f : f + 1],
+                )
+            grouped = work.tile([P, PASSES, B, PACK], BF16, align_bytes=64)
+            nc.scalar.copy(out=grouped[:], in_=h_planes[:].rearrange("p (g t) b -> p g b t", t=PACK))
+            codes = work.tile([P, PASSES * B], U32, align_bytes=64)
+            scales = work.tile([P, PASSES * B], U8, align_bytes=64)
+            nc.vector.quantize_mx(
+                out=codes[:].bitcast(FP8X4),
+                scales=scales[:],
+                in_=grouped[:].rearrange("p g b t -> p (g b t)"),
+            )
+            return codes, scales
+
+        def multiply(codes, scales, words, first_plane, n):
+            n_cols = slice(n * N_TILE, (n + 1) * N_TILE)
+            acc = psum_acc.tile([B, N_TILE], F32, name="acc")
+            for g in range(PASSES):
+                b_cols = slice(g * B, (g + 1) * B)
+                nc.tensor.matmul_mx(
+                    out=acc[:],
+                    lhsT=codes[:, b_cols].bitcast(FP8X4),
+                    lhsT_scale=scales[:, b_cols],
+                    rhs=words[:, g, n_cols].bitcast(FP8X4),
+                    rhs_scale=w_planes[first_plane + 4 * g : P, n_cols],
+                    start=(g == 0),
+                    stop=(g == PASSES - 1),
+                )
+            return acc
+
+        gate = keep.tile([B, N], F32)
+        gated_bias = keep.tile([B, N], F32)
+        codes, scales = hidden_layer(SLICES, c_z[:], c_gain, c_shift)
+        for n in range(N_TILES):
+            n_cols = slice(n * N_TILE, (n + 1) * N_TILE)
+            acc = multiply(codes, scales, c_words, 8, n)
+            nc.vector.tensor_tensor(out=gate[:, n_cols], in0=acc[:], in1=c_bias[:, n_cols], op=ALU.add)
+        nc.vector.tensor_tensor(out=gated_bias[:], in0=gate[:], in1=s_bias[:], op=ALU.mult)
+
+        running_max = keep.tile([B, STORE, N], F32)
+        for first in range(0, SLICES, STORE):
+            s_out = stores.tile([B, STORE, N], F32)
+            for j in range(STORE):
+                i = first + j
+                codes, scales = hidden_layer(i, s_z[i // LOAD][:, i % LOAD, :], s_gain, s_shift)
+                for n in range(N_TILES):
+                    n_cols = slice(n * N_TILE, (n + 1) * N_TILE)
+                    acc = multiply(codes, scales, s_words, 0, n)
+                    nc.vector.tensor_tensor(out=s_out[:, j, n_cols], in0=acc[:], in1=gate[:, n_cols], op=ALU.mult)
+            nc.vector.tensor_tensor(
+                out=s_out[:],
+                in0=s_out[:],
+                in1=gated_bias[:].unsqueeze(1).to_broadcast([B, STORE, N]),
+                op=ALU.add,
+            )
+            nc.sync.dma_start(out=out_0[:, first : first + STORE, :], in_=s_out[:])
+            if first == 0:
+                nc.vector.tensor_copy(out=running_max[:], in_=s_out[:])
+            else:
+                nc.vector.tensor_tensor(out=running_max[:], in0=running_max[:], in1=s_out[:], op=ALU.max)
+
+        pooled = keep.tile([B, N], F32)
+        nc.vector.tensor_tensor(out=pooled[:], in0=running_max[:, 0, :], in1=running_max[:, 1, :], op=ALU.max)
+        nc.sync.dma_start(out=out_1, in_=pooled[:])

@@ -15,6 +15,7 @@ ALU = mybir.AluOpType
 P = 128
 B = 128
 SLICES = 32
+UNITS = SLICES + 1
 K = 1024
 N = 1024
 PACK = 4
@@ -27,7 +28,7 @@ LOAD = 4
 STORE = 2
 EPS = 1e-5
 
-FLOPS = 2 * (SLICES + 1) * B * K * N
+FLOPS = 2 * UNITS * B * K * N
 
 
 def tile_cgblock_pb_kernel(
@@ -49,18 +50,16 @@ def tile_cgblock_pb_kernel(
 ):
     nc = tc.nc
     with ExitStack() as pools:
+        pools.enter_context(tc.manual_schedule())
         keep = pools.enter_context(tc.tile_pool(name="keep", bufs=1))
         small = pools.enter_context(tc.tile_pool(name="small", bufs=4))
         work = pools.enter_context(tc.tile_pool(name="work", bufs=3))
         stores = pools.enter_context(tc.tile_pool(name="stores", bufs=3))
-        psum_t = pools.enter_context(tc.psum_pool(name="psum_t", bufs=3))
-        psum_sum = pools.enter_context(tc.psum_pool(name="psum_sum", bufs=1))
+        psum_t = pools.enter_context(tc.psum_pool(name="psum_t", bufs=4))
         psum_acc = pools.enter_context(tc.psum_pool(name="psum_acc", bufs=4))
 
         ident = keep.tile([P, P], F32)
         make_identity(nc, ident[:])
-        ones = keep.tile([P, 1], BF16)
-        nc.vector.memset(ones[:], 1.0)
         eps = keep.tile([P, 1], F32)
         nc.vector.memset(eps[:], EPS)
 
@@ -114,122 +113,159 @@ def tile_cgblock_pb_kernel(
         s_bias = keep.tile([P, N], BF16)
         nc.scalar.dma_start(out=s_bias[:], in_=s_b3.partition_broadcast(P))
 
-        sums = psum_sum.tile([P, (SLICES + 1) * PLANES], F32)
+        z_t = {}
+        stats = {}
+        std = {}
+        slope = {}
+        offset = {}
+        h_planes = {}
+        grouped = {}
+        codes = {}
+        scales = {}
+        products = {}
 
-        def hidden_layer(unit, z_unit, gain, shift):
-            z_t = psum_t.tile([P, PASSES * 2, B], F32)
-            z_words = z_unit.bitcast(F32)
+        def z_of(unit):
+            if unit == 0:
+                return c_z[:]
+            i = unit - 1
+            return s_z[i // LOAD][:, i % LOAD, :]
+
+        def transpose(unit):
+            z_t[unit] = psum_t.tile([P, PASSES * 2, B], F32, name="z_t")
+            z_words = z_of(unit).bitcast(F32)
             for g in range(PASSES):
                 for h in range(2):
                     nc.tensor.transpose(
-                        z_t[:, 2 * g + h, :], z_words[:, 256 * g + h : 256 * (g + 1) : 2], ident[:]
+                        z_t[unit][:, 2 * g + h, :], z_words[:, 256 * g + h : 256 * (g + 1) : 2], ident[:]
                     )
-            unit_sums = sums[:, unit * PLANES : (unit + 1) * PLANES]
-            for g in range(PASSES):
-                for t in range(PACK):
-                    nc.tensor.matmul(
-                        unit_sums[:, PACK * g + t : PACK * g + t + 1],
-                        lhsT=z_unit[:, K_PASS * g + t : K_PASS * (g + 1) : PACK],
-                        rhs=ones[:],
-                        start=True,
-                        stop=True,
-                    )
-            halves = z_t[:].bitcast(BF16).rearrange("p q (b e) -> p q e b", e=2)
 
-            def plane(f):
-                return halves[:, f // 2, f % 2, :]
-
-            neg_mean = small.tile([P, PLANES], F32)
-            nc.scalar.mul(out=neg_mean[:], in_=unit_sums, mul=-1.0 / B)
-            squares = work.tile([P, PLANES, B], BF16)
-            sum_sq = small.tile([P, PLANES], F32)
-            for f in range(PLANES):
-                nc.scalar.activation(
-                    out=squares[:, f, :],
-                    in_=plane(f),
-                    func=ACT.Square,
-                    bias=neg_mean[:, f : f + 1],
-                    scale=1.0,
-                    accum_out=sum_sq[:, f : f + 1],
+        def statistics(unit):
+            stats[unit] = small.tile([P, PASSES * 2, 2, 3], F32, name="stats")
+            for q in range(PASSES * 2):
+                nc.vector.bn_stats(
+                    out=stats[unit][:, q, :, :].rearrange("p e s -> p (e s)"), in_=z_t[unit][:, q, :].bitcast(BF16)
                 )
-            std = small.tile([P, PLANES], F32)
-            nc.scalar.activation(out=std[:], in_=sum_sq[:], func=ACT.Sqrt, bias=eps[:], scale=1.0 / B)
-            rstd = small.tile([P, PLANES], F32)
-            nc.vector.reciprocal(out=rstd[:], in_=std[:])
-            slope = small.tile([P, PLANES], F32)
-            nc.gpsimd.tensor_tensor(out=slope[:], in0=rstd[:], in1=gain, op=ALU.mult)
-            centre = small.tile([P, PLANES], F32)
-            nc.gpsimd.tensor_tensor(out=centre[:], in0=slope[:], in1=neg_mean[:], op=ALU.mult)
-            offset = small.tile([P, PLANES], F32)
-            nc.gpsimd.tensor_tensor(out=offset[:], in0=centre[:], in1=shift, op=ALU.add)
 
-            h_planes = work.tile([P, PLANES, B], BF16)
-            for f in range(PLANES):
-                nc.scalar.activation(
-                    out=h_planes[:, f, :],
-                    in_=plane(f),
-                    func=ACT.Relu,
-                    bias=offset[:, f : f + 1],
-                    scale=slope[:, f : f + 1],
-                )
-            grouped = work.tile([P, PASSES, B, PACK], BF16, align_bytes=64)
-            nc.scalar.copy(out=grouped[:], in_=h_planes[:].rearrange("p (g t) b -> p g b t", t=PACK))
-            codes = work.tile([P, PASSES * B], U32, align_bytes=64)
-            scales = work.tile([P, PASSES * B], U8, align_bytes=64)
-            nc.vector.quantize_mx(
-                out=codes[:].bitcast(FP8X4),
-                scales=scales[:],
-                in_=grouped[:].rearrange("p g b t -> p (g b t)"),
+        def deviation(unit):
+            std[unit] = small.tile([P, PASSES * 2, 2], F32, name="std")
+            nc.scalar.activation(
+                out=std[unit][:], in_=stats[unit][:, :, :, 2], func=ACT.Sqrt, bias=eps[:], scale=1.0 / B
             )
-            return codes, scales
 
-        def multiply(codes, scales, words, first_plane, n):
-            n_cols = slice(n * N_TILE, (n + 1) * N_TILE)
-            acc = psum_acc.tile([B, N_TILE], F32, name="acc")
-            for g in range(PASSES):
-                b_cols = slice(g * B, (g + 1) * B)
-                nc.tensor.matmul_mx(
-                    out=acc[:],
-                    lhsT=codes[:, b_cols].bitcast(FP8X4),
-                    lhsT_scale=scales[:, b_cols],
-                    rhs=words[:, g, n_cols].bitcast(FP8X4),
-                    rhs_scale=w_planes[first_plane + 4 * g : P, n_cols],
-                    start=(g == 0),
-                    stop=(g == PASSES - 1),
+        def line(unit):
+            gain, shift = (c_gain, c_shift) if unit == 0 else (s_gain, s_shift)
+            rstd = small.tile([P, PLANES], F32)
+            nc.vector.reciprocal(out=rstd[:], in_=std[unit][:].rearrange("p q e -> p (q e)"))
+            slope[unit] = small.tile([P, PLANES], F32, name="slope")
+            nc.vector.tensor_tensor(out=slope[unit][:], in0=rstd[:], in1=gain, op=ALU.mult)
+            centre = small.tile([P, PLANES], F32)
+            nc.vector.tensor_tensor(
+                out=centre[:].rearrange("p (q e) -> p q e", e=2),
+                in0=slope[unit][:].rearrange("p (q e) -> p q e", e=2),
+                in1=stats[unit][:, :, :, 1],
+                op=ALU.mult,
+            )
+            offset[unit] = small.tile([P, PLANES], F32, name="offset")
+            nc.vector.tensor_tensor(out=offset[unit][:], in0=shift, in1=centre[:], op=ALU.subtract)
+
+        def normalise(unit):
+            halves = z_t[unit][:].bitcast(BF16).rearrange("p q (b e) -> p q e b", e=2)
+            h_planes[unit] = work.tile([P, PLANES, B], BF16, name="h_planes")
+            for f in range(PLANES):
+                nc.scalar.activation(
+                    out=h_planes[unit][:, f, :],
+                    in_=halves[:, f // 2, f % 2, :],
+                    func=ACT.Relu,
+                    bias=offset[unit][:, f : f + 1],
+                    scale=slope[unit][:, f : f + 1],
                 )
-            return acc
+
+        def regroup(unit):
+            grouped[unit] = work.tile([P, PASSES, B, PACK], BF16, name="grouped", align_bytes=64)
+            nc.scalar.copy(out=grouped[unit][:], in_=h_planes[unit][:].rearrange("p (g t) b -> p g b t", t=PACK))
+
+        def quantise(unit):
+            codes[unit] = work.tile([P, PASSES * B], U32, name="codes", align_bytes=64)
+            scales[unit] = work.tile([P, PASSES * B], U8, name="scales", align_bytes=64)
+            nc.vector.quantize_mx(
+                out=codes[unit][:].bitcast(FP8X4),
+                scales=scales[unit][:],
+                in_=grouped[unit][:].rearrange("p g b t -> p (g b t)"),
+            )
+
+        def multiply(unit):
+            words, first_plane = (c_words, 8) if unit == 0 else (s_words, 0)
+            products[unit] = []
+            for n in range(N_TILES):
+                n_cols = slice(n * N_TILE, (n + 1) * N_TILE)
+                acc = psum_acc.tile([B, N_TILE], F32, name="acc")
+                for g in range(PASSES):
+                    b_cols = slice(g * B, (g + 1) * B)
+                    nc.tensor.matmul_mx(
+                        out=acc[:],
+                        lhsT=codes[unit][:, b_cols].bitcast(FP8X4),
+                        lhsT_scale=scales[unit][:, b_cols],
+                        rhs=words[:, g, n_cols].bitcast(FP8X4),
+                        rhs_scale=w_planes[first_plane + 4 * g : P, n_cols],
+                        start=(g == 0),
+                        stop=(g == PASSES - 1),
+                    )
+                products[unit].append(acc)
 
         gate = keep.tile([B, N], F32)
         gated_bias = keep.tile([B, N], F32)
-        codes, scales = hidden_layer(SLICES, c_z[:], c_gain, c_shift)
-        for n in range(N_TILES):
-            n_cols = slice(n * N_TILE, (n + 1) * N_TILE)
-            acc = multiply(codes, scales, c_words, 8, n)
-            nc.vector.tensor_tensor(out=gate[:, n_cols], in0=acc[:], in1=c_bias[:, n_cols], op=ALU.add)
-        nc.vector.tensor_tensor(out=gated_bias[:], in0=gate[:], in1=s_bias[:], op=ALU.mult)
+        pooled = keep.tile([B, N], F32)
+        s_out = {}
 
-        running_max = keep.tile([B, STORE, N], F32)
-        for first in range(0, SLICES, STORE):
-            s_out = stores.tile([B, STORE, N], F32)
-            for j in range(STORE):
-                i = first + j
-                codes, scales = hidden_layer(i, s_z[i // LOAD][:, i % LOAD, :], s_gain, s_shift)
+        def this_slice(i):
+            return s_out[i - i % STORE][:, i % STORE, :]
+
+        def apply_gate(unit):
+            if unit == 0:
                 for n in range(N_TILES):
                     n_cols = slice(n * N_TILE, (n + 1) * N_TILE)
-                    acc = multiply(codes, scales, s_words, 0, n)
-                    nc.vector.tensor_tensor(out=s_out[:, j, n_cols], in0=acc[:], in1=gate[:, n_cols], op=ALU.mult)
-            nc.vector.tensor_tensor(
-                out=s_out[:],
-                in0=s_out[:],
-                in1=gated_bias[:].unsqueeze(1).to_broadcast([B, STORE, N]),
-                op=ALU.add,
-            )
-            nc.sync.dma_start(out=out_0[:, first : first + STORE, :], in_=s_out[:])
-            if first == 0:
-                nc.vector.tensor_copy(out=running_max[:], in_=s_out[:])
-            else:
-                nc.vector.tensor_tensor(out=running_max[:], in0=running_max[:], in1=s_out[:], op=ALU.max)
+                    nc.vector.tensor_tensor(
+                        out=gate[:, n_cols], in0=products[unit][n][:], in1=c_bias[:, n_cols], op=ALU.add
+                    )
+                return
+            i = unit - 1
+            if i % STORE == 0:
+                s_out[i] = stores.tile([B, STORE, N], F32, name="s_out")
+            for n in range(N_TILES):
+                n_cols = slice(n * N_TILE, (n + 1) * N_TILE)
+                nc.vector.tensor_tensor(
+                    out=this_slice(i)[:, n_cols], in0=products[unit][n][:], in1=gate[:, n_cols], op=ALU.mult
+                )
 
-        pooled = keep.tile([B, N], F32)
-        nc.vector.tensor_tensor(out=pooled[:], in0=running_max[:, 0, :], in1=running_max[:, 1, :], op=ALU.max)
+        def pool_and_store(unit):
+            if unit == 0:
+                nc.gpsimd.tensor_tensor(out=gated_bias[:], in0=gate[:], in1=s_bias[:], op=ALU.mult)
+                return
+            i = unit - 1
+            if i == 0:
+                nc.vector.tensor_copy(out=pooled[:], in_=this_slice(i))
+            else:
+                nc.vector.tensor_tensor(out=pooled[:], in0=pooled[:], in1=this_slice(i), op=ALU.max)
+            nc.gpsimd.tensor_tensor(out=this_slice(i), in0=this_slice(i), in1=gated_bias[:], op=ALU.add)
+            if i % STORE == STORE - 1:
+                first = i - i % STORE
+                nc.sync.dma_start(out=out_0[:, first : first + STORE, :], in_=s_out[first][:])
+
+        def stage(function, unit):
+            if 0 <= unit < UNITS:
+                function(unit)
+
+        for step in range(UNITS + 4):
+            stage(transpose, step)
+            stage(statistics, step - 1)
+            stage(normalise, step - 2)
+            stage(deviation, step - 1)
+            stage(regroup, step - 2)
+            stage(apply_gate, step - 4)
+            stage(quantise, step - 3)
+            stage(multiply, step - 3)
+            stage(line, step - 1)
+            stage(pool_and_store, step - 4)
+
+        nc.vector.tensor_tensor(out=pooled[:], in0=pooled[:], in1=gated_bias[:], op=ALU.add)
         nc.sync.dma_start(out=out_1, in_=pooled[:])

@@ -157,16 +157,16 @@ def tile_cgblock_pb_kernel(
             rstd = small.tile([P, PLANES], F32)
             nc.vector.reciprocal(out=rstd[:], in_=std[unit][:].rearrange("p q e -> p (q e)"))
             slope[unit] = small.tile([P, PLANES], F32, name="slope")
-            nc.vector.tensor_tensor(out=slope[unit][:], in0=rstd[:], in1=gain, op=ALU.mult)
+            nc.gpsimd.tensor_tensor(out=slope[unit][:], in0=rstd[:], in1=gain, op=ALU.mult)
             centre = small.tile([P, PLANES], F32)
-            nc.vector.tensor_tensor(
+            nc.gpsimd.tensor_tensor(
                 out=centre[:].rearrange("p (q e) -> p q e", e=2),
                 in0=slope[unit][:].rearrange("p (q e) -> p q e", e=2),
                 in1=stats[unit][:, :, :, 1],
                 op=ALU.mult,
             )
             offset[unit] = small.tile([P, PLANES], F32, name="offset")
-            nc.vector.tensor_tensor(out=offset[unit][:], in0=shift, in1=centre[:], op=ALU.subtract)
+            nc.gpsimd.tensor_tensor(out=offset[unit][:], in0=shift, in1=centre[:], op=ALU.subtract)
 
         def normalise(unit):
             halves = z_t[unit][:].bitcast(BF16).rearrange("p q (b e) -> p q e b", e=2)

@@ -255,17 +255,17 @@ def tile_cgblock_pb_kernel(
             if 0 <= unit < UNITS:
                 function(unit)
 
-        for step in range(UNITS + 4):
+        for step in range(UNITS + 5):
             stage(transpose, step)
             stage(statistics, step - 1)
-            stage(normalise, step - 2)
+            stage(normalise, step - 3)
             stage(deviation, step - 1)
-            stage(regroup, step - 2)
-            stage(apply_gate, step - 4)
-            stage(quantise, step - 3)
-            stage(multiply, step - 3)
+            stage(regroup, step - 3)
+            stage(apply_gate, step - 5)
+            stage(quantise, step - 4)
+            stage(multiply, step - 4)
             stage(line, step - 1)
-            stage(pool_and_store, step - 4)
+            stage(pool_and_store, step - 5)
 
         nc.vector.tensor_tensor(out=pooled[:], in0=pooled[:], in1=gated_bias[:], op=ALU.add)
         nc.sync.dma_start(out=out_1, in_=pooled[:])

@@ -26,6 +26,7 @@ N_TILE = 512
 N_TILES = N // N_TILE
 LOAD = 4
 STORE = 2
+GPSIMD_COLS = 512
 EPS = 1e-5
 
 FLOPS = 2 * UNITS * B * K * N
@@ -246,7 +247,14 @@ def tile_cgblock_pb_kernel(
                 nc.vector.tensor_copy(out=pooled[:], in_=this_slice(i))
             else:
                 nc.vector.tensor_tensor(out=pooled[:], in0=pooled[:], in1=this_slice(i), op=ALU.max)
-            nc.gpsimd.tensor_tensor(out=this_slice(i), in0=this_slice(i), in1=gated_bias[:], op=ALU.add)
+            lower = slice(0, N - GPSIMD_COLS)
+            upper = slice(N - GPSIMD_COLS, N)
+            nc.gpsimd.tensor_tensor(
+                out=this_slice(i)[:, upper], in0=this_slice(i)[:, upper], in1=gated_bias[:, upper], op=ALU.add
+            )
+            nc.vector.tensor_tensor(
+                out=this_slice(i)[:, lower], in0=this_slice(i)[:, lower], in1=gated_bias[:, lower], op=ALU.add
+            )
             if i % STORE == STORE - 1:
                 first = i - i % STORE
                 nc.sync.dma_start(out=out_0[:, first : first + STORE, :], in_=s_out[first][:])
@@ -257,6 +265,7 @@ def tile_cgblock_pb_kernel(
 
         for step in range(UNITS + 5):
             stage(transpose, step)
+            stage(line, step - 2)
             stage(statistics, step - 1)
             stage(normalise, step - 3)
             stage(deviation, step - 1)
@@ -264,7 +273,6 @@ def tile_cgblock_pb_kernel(
             stage(apply_gate, step - 5)
             stage(quantise, step - 4)
             stage(multiply, step - 4)
-            stage(line, step - 1)
             stage(pool_and_store, step - 5)
 
         nc.vector.tensor_tensor(out=pooled[:], in0=pooled[:], in1=gated_bias[:], op=ALU.add)

@@ -25,7 +25,6 @@ PLANES = PASSES * PACK
 N_TILE = 512
 N_TILES = N // N_TILE
 LOAD = 4
-STORE = 2
 GPSIMD_COLS = 512
 EPS = 1e-5
 
@@ -55,7 +54,7 @@ def tile_cgblock_pb_kernel(
         keep = pools.enter_context(tc.tile_pool(name="keep", bufs=1))
         small = pools.enter_context(tc.tile_pool(name="small", bufs=4))
         work = pools.enter_context(tc.tile_pool(name="work", bufs=3))
-        stores = pools.enter_context(tc.tile_pool(name="stores", bufs=3))
+        stores = pools.enter_context(tc.tile_pool(name="stores", bufs=5))
         psum_t = pools.enter_context(tc.psum_pool(name="psum_t", bufs=4))
         psum_acc = pools.enter_context(tc.psum_pool(name="psum_acc", bufs=4))
 
@@ -217,53 +216,50 @@ def tile_cgblock_pb_kernel(
         gated_bias = keep.tile([B, N], F32)
         pooled = keep.tile([B, N], F32)
         s_out = {}
-
-        def this_slice(i):
-            return s_out[i - i % STORE][:, i % STORE, :]
+        vector_cols = slice(0, N - GPSIMD_COLS)
+        gpsimd_cols = slice(N - GPSIMD_COLS, N)
 
         def apply_gate(unit):
             if unit == 0:
-                for n in range(N_TILES):
-                    n_cols = slice(n * N_TILE, (n + 1) * N_TILE)
-                    nc.vector.tensor_tensor(
-                        out=gate[:, n_cols], in0=products[unit][n][:], in1=c_bias[:, n_cols], op=ALU.add
-                    )
-                return
-            i = unit - 1
-            if i % STORE == 0:
-                s_out[i] = stores.tile([B, STORE, N], F32, name="s_out")
+                gated, other, op = gate, c_bias, ALU.add
+            else:
+                s_out[unit] = stores.tile([B, N], F32, name="s_out")
+                gated, other, op = s_out[unit], gate, ALU.mult
             for n in range(N_TILES):
                 n_cols = slice(n * N_TILE, (n + 1) * N_TILE)
-                nc.vector.tensor_tensor(
-                    out=this_slice(i)[:, n_cols], in0=products[unit][n][:], in1=gate[:, n_cols], op=ALU.mult
-                )
+                nc.vector.tensor_tensor(out=gated[:, n_cols], in0=products[unit][n][:], in1=other[:, n_cols], op=op)
 
-        def pool_and_store(unit):
+        def pool(unit):
             if unit == 0:
                 nc.gpsimd.tensor_tensor(out=gated_bias[:], in0=gate[:], in1=s_bias[:], op=ALU.mult)
                 return
-            i = unit - 1
-            if i == 0:
-                nc.vector.tensor_copy(out=pooled[:], in_=this_slice(i))
+            if unit == 1:
+                nc.vector.tensor_copy(out=pooled[:], in_=s_out[unit][:])
             else:
-                nc.vector.tensor_tensor(out=pooled[:], in0=pooled[:], in1=this_slice(i), op=ALU.max)
-            lower = slice(0, N - GPSIMD_COLS)
-            upper = slice(N - GPSIMD_COLS, N)
+                nc.vector.tensor_tensor(out=pooled[:], in0=pooled[:], in1=s_out[unit][:], op=ALU.max)
             nc.gpsimd.tensor_tensor(
-                out=this_slice(i)[:, upper], in0=this_slice(i)[:, upper], in1=gated_bias[:, upper], op=ALU.add
+                out=s_out[unit][:, gpsimd_cols],
+                in0=s_out[unit][:, gpsimd_cols],
+                in1=gated_bias[:, gpsimd_cols],
+                op=ALU.add,
             )
+
+        def finish(unit):
+            if unit == 0:
+                return
             nc.vector.tensor_tensor(
-                out=this_slice(i)[:, lower], in0=this_slice(i)[:, lower], in1=gated_bias[:, lower], op=ALU.add
+                out=s_out[unit][:, vector_cols],
+                in0=s_out[unit][:, vector_cols],
+                in1=gated_bias[:, vector_cols],
+                op=ALU.add,
             )
-            if i % STORE == STORE - 1:
-                first = i - i % STORE
-                nc.sync.dma_start(out=out_0[:, first : first + STORE, :], in_=s_out[first][:])
+            nc.sync.dma_start(out=out_0[:, unit - 1, :], in_=s_out[unit][:])
 
         def stage(function, unit):
             if 0 <= unit < UNITS:
                 function(unit)
 
-        for step in range(UNITS + 5):
+        for step in range(UNITS + 6):
             stage(transpose, step)
             stage(line, step - 2)
             stage(statistics, step - 1)
@@ -273,7 +269,8 @@ def tile_cgblock_pb_kernel(
             stage(apply_gate, step - 5)
             stage(quantise, step - 4)
             stage(multiply, step - 4)
-            stage(pool_and_store, step - 5)
+            stage(finish, step - 6)
+            stage(pool, step - 5)
 
         nc.vector.tensor_tensor(out=pooled[:], in0=pooled[:], in1=gated_bias[:], op=ALU.add)
         nc.sync.dma_start(out=out_1, in_=pooled[:])

@@ -21,12 +21,14 @@ N = 1024
 PACK = 4
 K_PASS = P * PACK
 PASSES = K // K_PASS
-PLANES = PASSES * PACK
+HELD = PASSES * PACK
+PAIRS = HELD // 2
 N_TILE = 512
 N_TILES = N // N_TILE
 LOAD = 4
-GPSIMD_COLS = 512
 EPS = 1e-5
+GPSIMD_COLS = 512
+LAST_LAG = 6
 
 FLOPS = 2 * UNITS * B * K * N
 
@@ -62,38 +64,8 @@ def tile_cgblock_pb_kernel(
         make_identity(nc, ident[:])
         eps = keep.tile([P, 1], F32)
         nc.vector.memset(eps[:], EPS)
-
-        c_z = keep.tile([P, K], BF16)
-        nc.sync.dma_start(out=c_z[:], in_=c_z2)
-
-        w_planes = keep.tile([P, N], U8, align_bytes=64)
-        nc.vector.memset(w_planes[:].bitcast(I32), 0)
-        for quadrant in range(4):
-            for w, w_scales in enumerate((s_w3_scales, c_w3_scales)):
-                first = 32 * quadrant + 8 * w
-                nc.sync.dma_start(
-                    out=w_planes[first : first + 8, :].bitcast(I32),
-                    in_=w_scales[:, 4 * quadrant : 4 * quadrant + 4, :].bitcast(I32),
-                )
-
-        def load_words(words_dram, name):
-            words = keep.tile([P, PASSES, N], U32, name=name, align_bytes=64)
-            nc.sync.dma_start(
-                out=words[:].bitcast(I32),
-                in_=words_dram.rearrange("g p n t -> p g (n t)").bitcast(I32),
-            )
-            return words
-
-        def load_slices(first):
-            z = keep.tile([P, LOAD, K], BF16, name="z%d" % first)
-            nc.sync.dma_start(out=z[:], in_=s_z2[:, first : first + LOAD, :])
-            return z
-
-        c_words = load_words(c_w3_words, "c_words")
-        s_z = [load_slices(0)]
-        s_words = load_words(s_w3_words, "s_words")
-        for first in range(LOAD, SLICES, LOAD):
-            s_z.append(load_slices(first))
+        warm = keep.tile([P, 1], F32)
+        nc.scalar.activation(out=warm[:], in_=eps[:], func=ACT.Sqrt)
 
         def load_by_feature(vector, name):
             by_feature = keep.tile([P, PASSES, PACK], BF16, name=name)
@@ -108,31 +80,58 @@ def tile_cgblock_pb_kernel(
         s_gain = load_by_feature(s_g2, "s_gain")
         s_shift = load_by_feature(s_be2, "s_shift")
 
-        c_bias = keep.tile([P, N], BF16)
-        nc.scalar.dma_start(out=c_bias[:], in_=c_b3.partition_broadcast(P))
-        s_bias = keep.tile([P, N], BF16)
-        nc.scalar.dma_start(out=s_bias[:], in_=s_b3.partition_broadcast(P))
+        c_z = keep.tile([B, K], BF16)
+        nc.sync.dma_start(out=c_z[:], in_=c_z2)
+
+        w_planes = keep.tile([P, N], U8, align_bytes=64)
+        nc.vector.memset(w_planes[:].bitcast(I32), 0)
+        for quadrant in range(4):
+            for first_plane, w_scales in ((0, s_w3_scales), (8, c_w3_scales)):
+                first = 32 * quadrant + first_plane
+                nc.sync.dma_start(
+                    out=w_planes[first : first + 4 * PASSES, :].bitcast(I32),
+                    in_=w_scales[:, 4 * quadrant : 4 * quadrant + 4, :].bitcast(I32),
+                )
+
+        def load_words(words_dram, name):
+            words = keep.tile([P, PASSES, N], U32, name=name, align_bytes=64)
+            nc.sync.dma_start(
+                out=words[:].bitcast(I32),
+                in_=words_dram.rearrange("g p n t -> p g (n t)").bitcast(I32),
+            )
+            return words
+
+        def load_slices(first):
+            z = keep.tile([B, LOAD, K], BF16, name="z%d" % first)
+            nc.sync.dma_start(out=z[:], in_=s_z2[:, first : first + LOAD, :])
+            return z
+
+        c_words = load_words(c_w3_words, "c_words")
+        s_z = [load_slices(0)]
+        s_words = load_words(s_w3_words, "s_words")
+        c_bias = keep.tile([B, N], BF16)
+        nc.sync.dma_start(out=c_bias[:], in_=c_b3.partition_broadcast(B))
+        s_bias = keep.tile([B, N], BF16)
+        nc.sync.dma_start(out=s_bias[:], in_=s_b3.partition_broadcast(B))
+        for first in range(LOAD, SLICES, LOAD):
+            s_z.append(load_slices(first))
 
         z_t = {}
         stats = {}
         std = {}
         slope = {}
         offset = {}
-        h_planes = {}
+        h_by_feature = {}
         grouped = {}
         codes = {}
         scales = {}
         products = {}
-
-        def z_of(unit):
-            if unit == 0:
-                return c_z[:]
-            i = unit - 1
-            return s_z[i // LOAD][:, i % LOAD, :]
+        s_out = {}
 
         def transpose(unit):
-            z_t[unit] = psum_t.tile([P, PASSES * 2, B], F32, name="z_t")
-            z_words = z_of(unit).bitcast(F32)
+            z = c_z[:] if unit == 0 else s_z[(unit - 1) // LOAD][:, (unit - 1) % LOAD, :]
+            z_words = z.bitcast(F32)
+            z_t[unit] = psum_t.tile([P, PAIRS, B], F32, name="z_t")
             for g in range(PASSES):
                 for h in range(2):
                     nc.tensor.transpose(
@@ -140,40 +139,41 @@ def tile_cgblock_pb_kernel(
                     )
 
         def statistics(unit):
-            stats[unit] = small.tile([P, PASSES * 2, 2, 3], F32, name="stats")
-            for q in range(PASSES * 2):
+            stats[unit] = small.tile([P, PAIRS, 2, 3], F32, name="stats")
+            for pair in range(PAIRS):
                 nc.vector.bn_stats(
-                    out=stats[unit][:, q, :, :].rearrange("p e s -> p (e s)"), in_=z_t[unit][:, q, :].bitcast(BF16)
+                    out=stats[unit][:, pair, :, :].rearrange("p e s -> p (e s)"),
+                    in_=z_t[unit][:, pair, :].bitcast(BF16),
                 )
 
         def deviation(unit):
-            std[unit] = small.tile([P, PASSES * 2, 2], F32, name="std")
+            std[unit] = small.tile([P, PAIRS, 2], F32, name="std")
             nc.scalar.activation(
                 out=std[unit][:], in_=stats[unit][:, :, :, 2], func=ACT.Sqrt, bias=eps[:], scale=1.0 / B
             )
 
         def line(unit):
             gain, shift = (c_gain, c_shift) if unit == 0 else (s_gain, s_shift)
-            rstd = small.tile([P, PLANES], F32)
+            rstd = small.tile([P, HELD], F32)
             nc.vector.reciprocal(out=rstd[:], in_=std[unit][:].rearrange("p q e -> p (q e)"))
-            slope[unit] = small.tile([P, PLANES], F32, name="slope")
+            slope[unit] = small.tile([P, HELD], F32, name="slope")
             nc.gpsimd.tensor_tensor(out=slope[unit][:], in0=rstd[:], in1=gain, op=ALU.mult)
-            centre = small.tile([P, PLANES], F32)
+            centre = small.tile([P, HELD], F32)
             nc.gpsimd.tensor_tensor(
                 out=centre[:].rearrange("p (q e) -> p q e", e=2),
                 in0=slope[unit][:].rearrange("p (q e) -> p q e", e=2),
                 in1=stats[unit][:, :, :, 1],
                 op=ALU.mult,
             )
-            offset[unit] = small.tile([P, PLANES], F32, name="offset")
+            offset[unit] = small.tile([P, HELD], F32, name="offset")
             nc.gpsimd.tensor_tensor(out=offset[unit][:], in0=shift, in1=centre[:], op=ALU.subtract)
 
         def normalise(unit):
             halves = z_t[unit][:].bitcast(BF16).rearrange("p q (b e) -> p q e b", e=2)
-            h_planes[unit] = work.tile([P, PLANES, B], BF16, name="h_planes")
-            for f in range(PLANES):
+            h_by_feature[unit] = work.tile([P, HELD, B], BF16, name="h_by_feature")
+            for f in range(HELD):
                 nc.scalar.activation(
-                    out=h_planes[unit][:, f, :],
+                    out=h_by_feature[unit][:, f, :],
                     in_=halves[:, f // 2, f % 2, :],
                     func=ACT.Relu,
                     bias=offset[unit][:, f : f + 1],
@@ -182,7 +182,9 @@ def tile_cgblock_pb_kernel(
 
         def regroup(unit):
             grouped[unit] = work.tile([P, PASSES, B, PACK], BF16, name="grouped", align_bytes=64)
-            nc.scalar.copy(out=grouped[unit][:], in_=h_planes[unit][:].rearrange("p (g t) b -> p g b t", t=PACK))
+            nc.scalar.copy(
+                out=grouped[unit][:], in_=h_by_feature[unit][:].rearrange("p (g t) b -> p g b t", t=PACK)
+            )
 
         def quantise(unit):
             codes[unit] = work.tile([P, PASSES * B], U32, name="codes", align_bytes=64)
@@ -215,7 +217,6 @@ def tile_cgblock_pb_kernel(
         gate = keep.tile([B, N], F32)
         gated_bias = keep.tile([B, N], F32)
         pooled = keep.tile([B, N], F32)
-        s_out = {}
         vector_cols = slice(0, N - GPSIMD_COLS)
         gpsimd_cols = slice(N - GPSIMD_COLS, N)
 
@@ -259,7 +260,7 @@ def tile_cgblock_pb_kernel(
             if 0 <= unit < UNITS:
                 function(unit)
 
-        for step in range(UNITS + 6):
+        for step in range(UNITS + LAST_LAG):
             stage(transpose, step)
             stage(line, step - 2)
             stage(statistics, step - 1)
@@ -269,7 +270,7 @@ def tile_cgblock_pb_kernel(
             stage(apply_gate, step - 5)
             stage(quantise, step - 4)
             stage(multiply, step - 4)
-            stage(finish, step - 6)
+            stage(finish, step - LAST_LAG)
             stage(pool, step - 5)
 
         nc.vector.tensor_tensor(out=pooled[:], in0=pooled[:], in1=gated_bias[:], op=ALU.add)

@@ -29,6 +29,7 @@ LOAD = 4
 EPS = 1e-5
 GPSIMD_COLS = 512
 LAST_LAG = 6
+VECTOR_PAIRS = 2
 
 FLOPS = 2 * UNITS * B * K * N
 
@@ -58,12 +59,16 @@ def tile_cgblock_pb_kernel(
         work = pools.enter_context(tc.tile_pool(name="work", bufs=3))
         stores = pools.enter_context(tc.tile_pool(name="stores", bufs=5))
         psum_t = pools.enter_context(tc.psum_pool(name="psum_t", bufs=4))
-        psum_acc = pools.enter_context(tc.psum_pool(name="psum_acc", bufs=4))
+        psum_acc = pools.enter_context(tc.psum_pool(name="psum_acc", bufs=3))
+        psum_sums = pools.enter_context(tc.psum_pool(name="psum_sums", bufs=1))
 
         ident = keep.tile([P, P], F32)
         make_identity(nc, ident[:])
         eps = keep.tile([P, 1], F32)
         nc.vector.memset(eps[:], EPS)
+        ones = keep.tile([B, 1], BF16)
+        nc.vector.memset(ones[:], 1.0)
+        squares = keep.tile([P, B], BF16)
         warm = keep.tile([P, 1], F32)
         nc.scalar.activation(out=warm[:], in_=eps[:], func=ACT.Sqrt)
 
@@ -117,6 +122,7 @@ def tile_cgblock_pb_kernel(
             s_z.append(load_slices(first))
 
         z_t = {}
+        sums = {}
         stats = {}
         std = {}
         slope = {}
@@ -138,9 +144,43 @@ def tile_cgblock_pb_kernel(
                         z_t[unit][:, 2 * g + h, :], z_words[:, 256 * g + h : 256 * (g + 1) : 2], ident[:]
                     )
 
+        def add_up(unit):
+            z = c_z[:] if unit == 0 else s_z[(unit - 1) // LOAD][:, (unit - 1) % LOAD, :]
+            sums[unit] = psum_sums.tile([P, HELD - 2 * VECTOR_PAIRS], F32, name="sums")
+            for f in range(2 * VECTOR_PAIRS, HELD):
+                g, t = divmod(f, PACK)
+                j = f - 2 * VECTOR_PAIRS
+                nc.tensor.matmul(
+                    out=sums[unit][:, j : j + 1],
+                    lhsT=z[:, K_PASS * g + t : K_PASS * (g + 1) : PACK],
+                    rhs=ones[:],
+                    start=True,
+                    stop=True,
+                )
+
+        def mean(unit):
+            nc.scalar.activation(
+                out=stats[unit][:, VECTOR_PAIRS:, :, 1],
+                in_=sums[unit][:].rearrange("p (q e) -> p q e", e=2),
+                func=ACT.Copy,
+                scale=1.0 / B,
+            )
+
+        def spread(unit):
+            halves = z_t[unit][:].bitcast(BF16).rearrange("p q (b e) -> p q e b", e=2)
+            for f in range(2 * VECTOR_PAIRS, HELD):
+                nc.scalar.activation(
+                    out=squares[:],
+                    in_=halves[:, f // 2, f % 2, :],
+                    func=ACT.Square,
+                    bias=stats[unit][:, f // 2, f % 2, 1:2],
+                    scale=-1.0,
+                    accum_out=stats[unit][:, f // 2, f % 2, 2:3],
+                )
+
         def statistics(unit):
             stats[unit] = small.tile([P, PAIRS, 2, 3], F32, name="stats")
-            for pair in range(PAIRS):
+            for pair in range(VECTOR_PAIRS):
                 nc.vector.bn_stats(
                     out=stats[unit][:, pair, :, :].rearrange("p e s -> p (e s)"),
                     in_=z_t[unit][:, pair, :].bitcast(BF16),
@@ -262,9 +302,12 @@ def tile_cgblock_pb_kernel(
 
         for step in range(UNITS + LAST_LAG):
             stage(transpose, step)
+            stage(add_up, step)
             stage(line, step - 2)
             stage(statistics, step - 1)
+            stage(mean, step - 1)
             stage(normalise, step - 3)
+            stage(spread, step - 1)
             stage(deviation, step - 1)
             stage(regroup, step - 3)
             stage(apply_gate, step - 5)

@@ -29,7 +29,7 @@ LOAD = 4
 EPS = 1e-5
 GPSIMD_COLS = 512
 LAST_LAG = 6
-VECTOR_PAIRS = 2
+VECTOR_PAIRS = 3
 
 FLOPS = 2 * UNITS * B * K * N
 

@@ -27,7 +27,7 @@ N_TILE = 512
 N_TILES = N // N_TILE
 LOAD = 4
 EPS = 1e-5
-GPSIMD_COLS = 512
+GPSIMD_COLS = 640
 LAST_LAG = 6
 VECTOR_PAIRS = 3
 
@@ -59,7 +59,8 @@ def tile_cgblock_pb_kernel(
         work = pools.enter_context(tc.tile_pool(name="work", bufs=3))
         stores = pools.enter_context(tc.tile_pool(name="stores", bufs=5))
         psum_t = pools.enter_context(tc.psum_pool(name="psum_t", bufs=4))
-        psum_acc = pools.enter_context(tc.psum_pool(name="psum_acc", bufs=3))
+        psum_acc = pools.enter_context(tc.psum_pool(name="psum_acc", bufs=2))
+        psum_bias = pools.enter_context(tc.psum_pool(name="psum_bias", bufs=1))
         psum_sums = pools.enter_context(tc.psum_pool(name="psum_sums", bufs=1))
 
         ident = keep.tile([P, P], F32)
@@ -87,6 +88,8 @@ def tile_cgblock_pb_kernel(
 
         c_z = keep.tile([B, K], BF16)
         nc.sync.dma_start(out=c_z[:], in_=c_z2)
+        z_first = keep.tile([B, LOAD, K], BF16)
+        nc.sync.dma_start(out=z_first[:, :2, :], in_=s_z2[:, :2, :])
 
         w_planes = keep.tile([P, N], U8, align_bytes=64)
         nc.vector.memset(w_planes[:].bitcast(I32), 0)
@@ -112,7 +115,8 @@ def tile_cgblock_pb_kernel(
             return z
 
         c_words = load_words(c_w3_words, "c_words")
-        s_z = [load_slices(0)]
+        nc.sync.dma_start(out=z_first[:, 2:, :], in_=s_z2[:, 2:LOAD, :])
+        s_z = [z_first]
         s_words = load_words(s_w3_words, "s_words")
         c_bias = keep.tile([B, N], BF16)
         nc.sync.dma_start(out=c_bias[:], in_=c_b3.partition_broadcast(B))
@@ -285,13 +289,18 @@ def tile_cgblock_pb_kernel(
                 op=ALU.add,
             )
 
+        bias_bank = psum_bias.tile([B, N - GPSIMD_COLS], F32)
+
+        def bank_bias():
+            nc.tensor.matmul(out=bias_bank[:], lhsT=ident[:], rhs=gated_bias[:, vector_cols], start=True, stop=True)
+
         def finish(unit):
             if unit == 0:
                 return
             nc.vector.tensor_tensor(
                 out=s_out[unit][:, vector_cols],
                 in0=s_out[unit][:, vector_cols],
-                in1=gated_bias[:, vector_cols],
+                in1=bias_bank[:],
                 op=ALU.add,
             )
             nc.sync.dma_start(out=out_0[:, unit - 1, :], in_=s_out[unit][:])
@@ -303,8 +312,11 @@ def tile_cgblock_pb_kernel(
         for step in range(UNITS + LAST_LAG):
             stage(transpose, step)
             stage(add_up, step)
+            if step == LAST_LAG:
+                bank_bias()
             stage(line, step - 2)
             stage(statistics, step - 1)
+            stage(finish, step - LAST_LAG)
             stage(mean, step - 1)
             stage(normalise, step - 3)
             stage(spread, step - 1)
@@ -313,7 +325,6 @@ def tile_cgblock_pb_kernel(
             stage(apply_gate, step - 5)
             stage(quantise, step - 4)
             stage(multiply, step - 4)
-            stage(finish, step - LAST_LAG)
             stage(pool, step - 5)
 
         nc.vector.tensor_tensor(out=pooled[:], in0=pooled[:], in1=gated_bias[:], op=ALU.add)

@@ -27,8 +27,8 @@ N_TILE = 512
 N_TILES = N // N_TILE
 LOAD = 4
 EPS = 1e-5
-GPSIMD_COLS = 640
-LAST_LAG = 6
+GPSIMD_COLS = 896
+LAST_LAG = 5
 VECTOR_PAIRS = 3
 
 FLOPS = 2 * UNITS * B * K * N
@@ -58,10 +58,10 @@ def tile_cgblock_pb_kernel(
         small = pools.enter_context(tc.tile_pool(name="small", bufs=4))
         work = pools.enter_context(tc.tile_pool(name="work", bufs=3))
         stores = pools.enter_context(tc.tile_pool(name="stores", bufs=5))
-        psum_t = pools.enter_context(tc.psum_pool(name="psum_t", bufs=4))
+        psum_t = pools.enter_context(tc.psum_pool(name="psum_t", bufs=3))
         psum_acc = pools.enter_context(tc.psum_pool(name="psum_acc", bufs=2))
         psum_bias = pools.enter_context(tc.psum_pool(name="psum_bias", bufs=1))
-        psum_sums = pools.enter_context(tc.psum_pool(name="psum_sums", bufs=1))
+        psum_sums = pools.enter_context(tc.psum_pool(name="psum_sums", bufs=2))
 
         ident = keep.tile([P, P], F32)
         make_identity(nc, ident[:])
@@ -182,13 +182,24 @@ def tile_cgblock_pb_kernel(
                     accum_out=stats[unit][:, f // 2, f % 2, 2:3],
                 )
 
+        def statistics_and_line(unit, line_unit):
+            line_steps = line(line_unit) if 0 <= line_unit < UNITS else []
+            stats_steps = statistics(unit) if 0 <= unit < UNITS else []
+            for i in range(max(len(line_steps), len(stats_steps))):
+                for steps in (line_steps, stats_steps):
+                    if i < len(steps):
+                        steps[i]()
+
         def statistics(unit):
             stats[unit] = small.tile([P, PAIRS, 2, 3], F32, name="stats")
-            for pair in range(VECTOR_PAIRS):
-                nc.vector.bn_stats(
+
+            def of_pair(pair):
+                return lambda: nc.vector.bn_stats(
                     out=stats[unit][:, pair, :, :].rearrange("p e s -> p (e s)"),
                     in_=z_t[unit][:, pair, :].bitcast(BF16),
                 )
+
+            return [of_pair(pair) for pair in range(VECTOR_PAIRS)]
 
         def deviation(unit):
             std[unit] = small.tile([P, PAIRS, 2], F32, name="std")
@@ -198,19 +209,21 @@ def tile_cgblock_pb_kernel(
 
         def line(unit):
             gain, shift = (c_gain, c_shift) if unit == 0 else (s_gain, s_shift)
-            rstd = small.tile([P, HELD], F32)
-            nc.vector.reciprocal(out=rstd[:], in_=std[unit][:].rearrange("p q e -> p (q e)"))
+            rstd = small.tile([P, HELD], F32, name="rstd")
             slope[unit] = small.tile([P, HELD], F32, name="slope")
-            nc.gpsimd.tensor_tensor(out=slope[unit][:], in0=rstd[:], in1=gain, op=ALU.mult)
-            centre = small.tile([P, HELD], F32)
-            nc.gpsimd.tensor_tensor(
-                out=centre[:].rearrange("p (q e) -> p q e", e=2),
-                in0=slope[unit][:].rearrange("p (q e) -> p q e", e=2),
-                in1=stats[unit][:, :, :, 1],
-                op=ALU.mult,
-            )
+            centre = small.tile([P, HELD], F32, name="centre")
             offset[unit] = small.tile([P, HELD], F32, name="offset")
-            nc.gpsimd.tensor_tensor(out=offset[unit][:], in0=shift, in1=centre[:], op=ALU.subtract)
+            return [
+                lambda: nc.vector.reciprocal(out=rstd[:], in_=std[unit][:].rearrange("p q e -> p (q e)")),
+                lambda: nc.vector.tensor_tensor(out=slope[unit][:], in0=rstd[:], in1=gain, op=ALU.mult),
+                lambda: nc.vector.tensor_tensor(
+                    out=centre[:].rearrange("p (q e) -> p q e", e=2),
+                    in0=slope[unit][:].rearrange("p (q e) -> p q e", e=2),
+                    in1=stats[unit][:, :, :, 1],
+                    op=ALU.mult,
+                ),
+                lambda: nc.vector.tensor_tensor(out=offset[unit][:], in0=shift, in1=centre[:], op=ALU.subtract),
+            ]
 
         def normalise(unit):
             halves = z_t[unit][:].bitcast(BF16).rearrange("p q (b e) -> p q e b", e=2)
@@ -282,12 +295,15 @@ def tile_cgblock_pb_kernel(
                 nc.vector.tensor_copy(out=pooled[:], in_=s_out[unit][:])
             else:
                 nc.vector.tensor_tensor(out=pooled[:], in0=pooled[:], in1=s_out[unit][:], op=ALU.max)
-            nc.gpsimd.tensor_tensor(
-                out=s_out[unit][:, gpsimd_cols],
-                in0=s_out[unit][:, gpsimd_cols],
-                in1=gated_bias[:, gpsimd_cols],
-                op=ALU.add,
-            )
+
+        def add_bias(unit):
+            if unit > 0:
+                nc.gpsimd.tensor_tensor(
+                    out=s_out[unit][:, gpsimd_cols],
+                    in0=s_out[unit][:, gpsimd_cols],
+                    in1=gated_bias[:, gpsimd_cols],
+                    op=ALU.add,
+                )
 
         bias_bank = psum_bias.tile([B, N - GPSIMD_COLS], F32)
 
@@ -314,18 +330,18 @@ def tile_cgblock_pb_kernel(
             stage(add_up, step)
             if step == LAST_LAG:
                 bank_bias()
-            stage(line, step - 2)
-            stage(statistics, step - 1)
+            statistics_and_line(step - 1, step - 2)
+            stage(add_bias, step - LAST_LAG)
             stage(finish, step - LAST_LAG)
+            stage(regroup, step - 3)
             stage(mean, step - 1)
-            stage(normalise, step - 3)
             stage(spread, step - 1)
             stage(deviation, step - 1)
-            stage(regroup, step - 3)
-            stage(apply_gate, step - 5)
-            stage(quantise, step - 4)
-            stage(multiply, step - 4)
-            stage(pool, step - 5)
+            stage(normalise, step - 2)
+            stage(apply_gate, step - 4)
+            stage(quantise, step - 3)
+            stage(multiply, step - 3)
+            stage(pool, step - 4)
 
         nc.vector.tensor_tensor(out=pooled[:], in0=pooled[:], in1=gated_bias[:], op=ALU.add)
         nc.sync.dma_start(out=out_1, in_=pooled[:])

@@ -26,9 +26,10 @@ PAIRS = HELD // 2
 N_TILE = 512
 N_TILES = N // N_TILE
 LOAD = 4
+GROUP = 2
 EPS = 1e-5
 GPSIMD_COLS = 896
-LAST_LAG = 5
+LAST_LAG = 6
 VECTOR_PAIRS = 3
 
 FLOPS = 2 * UNITS * B * K * N
@@ -58,10 +59,10 @@ def tile_cgblock_pb_kernel(
         small = pools.enter_context(tc.tile_pool(name="small", bufs=4))
         work = pools.enter_context(tc.tile_pool(name="work", bufs=3))
         stores = pools.enter_context(tc.tile_pool(name="stores", bufs=5))
-        psum_t = pools.enter_context(tc.psum_pool(name="psum_t", bufs=3))
+        psum_t = pools.enter_context(tc.psum_pool(name="psum_t", bufs=4))
         psum_acc = pools.enter_context(tc.psum_pool(name="psum_acc", bufs=2))
         psum_bias = pools.enter_context(tc.psum_pool(name="psum_bias", bufs=1))
-        psum_sums = pools.enter_context(tc.psum_pool(name="psum_sums", bufs=2))
+        psum_sums = pools.enter_context(tc.psum_pool(name="psum_sums", bufs=1))
 
         ident = keep.tile([P, P], F32)
         make_identity(nc, ident[:])
@@ -129,6 +130,8 @@ def tile_cgblock_pb_kernel(
         sums = {}
         stats = {}
         std = {}
+        rstd = {}
+        centre = {}
         slope = {}
         offset = {}
         h_by_feature = {}
@@ -162,9 +165,24 @@ def tile_cgblock_pb_kernel(
                     stop=True,
                 )
 
+        def place(unit):
+            first = unit if unit == 0 else unit - (unit - 1) % GROUP
+            return first, unit - first
+
+        def width(first):
+            return 1 if first == 0 else GROUP
+
+        def closes_group(unit):
+            first, i = place(unit)
+            return i == width(first) - 1
+
+        def unit_stats(unit):
+            first, i = place(unit)
+            return stats[first][:, i, :, :, :]
+
         def mean(unit):
             nc.scalar.activation(
-                out=stats[unit][:, VECTOR_PAIRS:, :, 1],
+                out=unit_stats(unit)[:, VECTOR_PAIRS:, :, 1],
                 in_=sums[unit][:].rearrange("p (q e) -> p q e", e=2),
                 func=ACT.Copy,
                 scale=1.0 / B,
@@ -177,64 +195,89 @@ def tile_cgblock_pb_kernel(
                     out=squares[:],
                     in_=halves[:, f // 2, f % 2, :],
                     func=ACT.Square,
-                    bias=stats[unit][:, f // 2, f % 2, 1:2],
+                    bias=unit_stats(unit)[:, f // 2, f % 2, 1:2],
                     scale=-1.0,
-                    accum_out=stats[unit][:, f // 2, f % 2, 2:3],
+                    accum_out=unit_stats(unit)[:, f // 2, f % 2, 2:3],
                 )
 
-        def statistics_and_line(unit, line_unit):
-            line_steps = line(line_unit) if 0 <= line_unit < UNITS else []
-            stats_steps = statistics(unit) if 0 <= unit < UNITS else []
-            for i in range(max(len(line_steps), len(stats_steps))):
-                for steps in (line_steps, stats_steps):
-                    if i < len(steps):
-                        steps[i]()
-
         def statistics(unit):
-            stats[unit] = small.tile([P, PAIRS, 2, 3], F32, name="stats")
-
-            def of_pair(pair):
-                return lambda: nc.vector.bn_stats(
-                    out=stats[unit][:, pair, :, :].rearrange("p e s -> p (e s)"),
+            first, i = place(unit)
+            if i == 0:
+                stats[first] = small.tile([P, GROUP, PAIRS, 2, 3], F32, name="stats")
+            for pair in range(VECTOR_PAIRS):
+                nc.vector.bn_stats(
+                    out=unit_stats(unit)[:, pair, :, :].rearrange("p e s -> p (e s)"),
                     in_=z_t[unit][:, pair, :].bitcast(BF16),
                 )
 
-            return [of_pair(pair) for pair in range(VECTOR_PAIRS)]
+        def by_unit(tile, first):
+            return tile[:, : width(first), :]
+
+        def repeated(vector, first):
+            return vector.unsqueeze(1).to_broadcast([P, width(first), HELD])
 
         def deviation(unit):
-            std[unit] = small.tile([P, PAIRS, 2], F32, name="std")
-            nc.scalar.activation(
-                out=std[unit][:], in_=stats[unit][:, :, :, 2], func=ACT.Sqrt, bias=eps[:], scale=1.0 / B
-            )
+            if closes_group(unit):
+                first = place(unit)[0]
+                std[first] = small.tile([P, GROUP, HELD], F32, name="std")
+                nc.scalar.activation(
+                    out=by_unit(std[first], first),
+                    in_=stats[first][:, : width(first), :, :, 2].rearrange("p i q e -> p i (q e)"),
+                    func=ACT.Sqrt,
+                    bias=eps[:],
+                    scale=1.0 / B,
+                )
 
-        def line(unit):
-            gain, shift = (c_gain, c_shift) if unit == 0 else (s_gain, s_shift)
-            rstd = small.tile([P, HELD], F32, name="rstd")
-            slope[unit] = small.tile([P, HELD], F32, name="slope")
-            centre = small.tile([P, HELD], F32, name="centre")
-            offset[unit] = small.tile([P, HELD], F32, name="offset")
-            return [
-                lambda: nc.vector.reciprocal(out=rstd[:], in_=std[unit][:].rearrange("p q e -> p (q e)")),
-                lambda: nc.vector.tensor_tensor(out=slope[unit][:], in0=rstd[:], in1=gain, op=ALU.mult),
-                lambda: nc.vector.tensor_tensor(
-                    out=centre[:].rearrange("p (q e) -> p q e", e=2),
-                    in0=slope[unit][:].rearrange("p (q e) -> p q e", e=2),
-                    in1=stats[unit][:, :, :, 1],
+        def invert(unit):
+            if closes_group(unit):
+                first = place(unit)[0]
+                rstd[first] = small.tile([P, GROUP, HELD], F32, name="rstd")
+                nc.vector.reciprocal(out=by_unit(rstd[first], first), in_=by_unit(std[first], first))
+
+        def make_slope(unit):
+            if closes_group(unit):
+                first = place(unit)[0]
+                slope[first] = small.tile([P, GROUP, HELD], F32, name="slope")
+                nc.vector.tensor_tensor(
+                    out=by_unit(slope[first], first),
+                    in0=by_unit(rstd[first], first),
+                    in1=repeated(c_gain if first == 0 else s_gain, first),
                     op=ALU.mult,
-                ),
-                lambda: nc.vector.tensor_tensor(out=offset[unit][:], in0=shift, in1=centre[:], op=ALU.subtract),
-            ]
+                )
+
+        def make_centre(unit):
+            if closes_group(unit):
+                first = place(unit)[0]
+                centre[first] = small.tile([P, GROUP, HELD], F32, name="centre")
+                nc.vector.tensor_tensor(
+                    out=by_unit(centre[first], first),
+                    in0=by_unit(slope[first], first),
+                    in1=stats[first][:, : width(first), :, :, 1].rearrange("p i q e -> p i (q e)"),
+                    op=ALU.mult,
+                )
+
+        def make_offset(unit):
+            if closes_group(unit):
+                first = place(unit)[0]
+                offset[first] = small.tile([P, GROUP, HELD], F32, name="offset")
+                nc.vector.tensor_tensor(
+                    out=by_unit(offset[first], first),
+                    in0=repeated(c_shift if first == 0 else s_shift, first),
+                    in1=by_unit(centre[first], first),
+                    op=ALU.subtract,
+                )
 
         def normalise(unit):
             halves = z_t[unit][:].bitcast(BF16).rearrange("p q (b e) -> p q e b", e=2)
+            first, i = place(unit)
             h_by_feature[unit] = work.tile([P, HELD, B], BF16, name="h_by_feature")
             for f in range(HELD):
                 nc.scalar.activation(
                     out=h_by_feature[unit][:, f, :],
                     in_=halves[:, f // 2, f % 2, :],
                     func=ACT.Relu,
-                    bias=offset[unit][:, f : f + 1],
-                    scale=slope[unit][:, f : f + 1],
+                    bias=offset[first][:, i, f : f + 1],
+                    scale=slope[first][:, i, f : f + 1],
                 )
 
         def regroup(unit):
@@ -277,15 +320,15 @@ def tile_cgblock_pb_kernel(
         vector_cols = slice(0, N - GPSIMD_COLS)
         gpsimd_cols = slice(N - GPSIMD_COLS, N)
 
-        def apply_gate(unit):
+        def apply_gate(unit, n):
             if unit == 0:
                 gated, other, op = gate, c_bias, ALU.add
             else:
-                s_out[unit] = stores.tile([B, N], F32, name="s_out")
+                if n == 0:
+                    s_out[unit] = stores.tile([B, N], F32, name="s_out")
                 gated, other, op = s_out[unit], gate, ALU.mult
-            for n in range(N_TILES):
-                n_cols = slice(n * N_TILE, (n + 1) * N_TILE)
-                nc.vector.tensor_tensor(out=gated[:, n_cols], in0=products[unit][n][:], in1=other[:, n_cols], op=op)
+            n_cols = slice(n * N_TILE, (n + 1) * N_TILE)
+            nc.vector.tensor_tensor(out=gated[:, n_cols], in0=products[unit][n][:], in1=other[:, n_cols], op=op)
 
         def pool(unit):
             if unit == 0:
@@ -321,27 +364,32 @@ def tile_cgblock_pb_kernel(
             )
             nc.sync.dma_start(out=out_0[:, unit - 1, :], in_=s_out[unit][:])
 
-        def stage(function, unit):
+        def stage(function, unit, *more):
             if 0 <= unit < UNITS:
-                function(unit)
+                function(unit, *more)
 
         for step in range(UNITS + LAST_LAG):
             stage(transpose, step)
             stage(add_up, step)
             if step == LAST_LAG:
                 bank_bias()
-            statistics_and_line(step - 1, step - 2)
+            stage(statistics, step - 1)
             stage(add_bias, step - LAST_LAG)
-            stage(finish, step - LAST_LAG)
-            stage(regroup, step - 3)
             stage(mean, step - 1)
             stage(spread, step - 1)
             stage(deviation, step - 1)
-            stage(normalise, step - 2)
-            stage(apply_gate, step - 4)
-            stage(quantise, step - 3)
-            stage(multiply, step - 3)
-            stage(pool, step - 4)
+            stage(normalise, step - 3)
+            stage(regroup, step - 3)
+            stage(apply_gate, step - 5, 0)
+            stage(apply_gate, step - 5, 1)
+            stage(invert, step - 1)
+            stage(finish, step - LAST_LAG)
+            stage(make_slope, step - 1)
+            stage(quantise, step - 4)
+            stage(multiply, step - 4)
+            stage(make_centre, step - 1)
+            stage(pool, step - 5)
+            stage(make_offset, step - 1)
 
         nc.vector.tensor_tensor(out=pooled[:], in0=pooled[:], in1=gated_bias[:], op=ALU.add)
         nc.sync.dma_start(out=out_1, in_=pooled[:])

@@ -28,9 +28,12 @@ N_TILES = N // N_TILE
 LOAD = 4
 GROUP = 2
 EPS = 1e-5
-GPSIMD_COLS = 896
+GPSIMD_COLS = 736
+LAST_GPSIMD_COLS = 512
+LAST_SLICES = 4
 LAST_LAG = 6
 VECTOR_PAIRS = 3
+FULL_UNITS = 5
 
 FLOPS = 2 * UNITS * B * K * N
 
@@ -91,6 +94,7 @@ def tile_cgblock_pb_kernel(
         nc.sync.dma_start(out=c_z[:], in_=c_z2)
         z_first = keep.tile([B, LOAD, K], BF16)
         nc.sync.dma_start(out=z_first[:, :2, :], in_=s_z2[:, :2, :])
+        nc.sync.dma_start(out=z_first[:, 2:, :], in_=s_z2[:, 2:LOAD, :])
 
         w_planes = keep.tile([P, N], U8, align_bytes=64)
         nc.vector.memset(w_planes[:].bitcast(I32), 0)
@@ -102,6 +106,12 @@ def tile_cgblock_pb_kernel(
                     in_=w_scales[:, 4 * quadrant : 4 * quadrant + 4, :].bitcast(I32),
                 )
 
+        def load_slices(first, count):
+            i = first % LOAD
+            nc.sync.dma_start(
+                out=s_z[first // LOAD][:, i : i + count, :], in_=s_z2[:, first : first + count, :]
+            )
+
         def load_words(words_dram, name):
             words = keep.tile([P, PASSES, N], U32, name=name, align_bytes=64)
             nc.sync.dma_start(
@@ -110,21 +120,22 @@ def tile_cgblock_pb_kernel(
             )
             return words
 
-        def load_slices(first):
-            z = keep.tile([B, LOAD, K], BF16, name="z%d" % first)
-            nc.sync.dma_start(out=z[:], in_=s_z2[:, first : first + LOAD, :])
-            return z
+        def load_bias(vector, name):
+            bias = keep.tile([B, N], BF16, name=name)
+            nc.sync.dma_start(out=bias[:], in_=vector.partition_broadcast(B))
+            return bias
 
         c_words = load_words(c_w3_words, "c_words")
-        nc.sync.dma_start(out=z_first[:, 2:, :], in_=s_z2[:, 2:LOAD, :])
-        s_z = [z_first]
+        c_bias = load_bias(c_b3, "c_bias")
+        s_z = []
+        for first in range(0, SLICES, LOAD):
+            s_z.append(z_first if first == 0 else keep.tile([B, LOAD, K], BF16, name="z%d" % first))
+        load_slices(4, 2)
         s_words = load_words(s_w3_words, "s_words")
-        c_bias = keep.tile([B, N], BF16)
-        nc.sync.dma_start(out=c_bias[:], in_=c_b3.partition_broadcast(B))
-        s_bias = keep.tile([B, N], BF16)
-        nc.sync.dma_start(out=s_bias[:], in_=s_b3.partition_broadcast(B))
-        for first in range(LOAD, SLICES, LOAD):
-            s_z.append(load_slices(first))
+        s_bias = load_bias(s_b3, "s_bias")
+        load_slices(6, 2)
+        for first in range(2 * LOAD, SLICES, LOAD):
+            load_slices(first, LOAD)
 
         z_t = {}
         sums = {}
@@ -151,8 +162,13 @@ def tile_cgblock_pb_kernel(
                         z_t[unit][:, 2 * g + h, :], z_words[:, 256 * g + h : 256 * (g + 1) : 2], ident[:]
                     )
 
+        def vector_pairs(unit):
+            return PAIRS if unit < FULL_UNITS else VECTOR_PAIRS
+
         def add_up(unit):
             z = c_z[:] if unit == 0 else s_z[(unit - 1) // LOAD][:, (unit - 1) % LOAD, :]
+            if vector_pairs(unit) == PAIRS:
+                return
             sums[unit] = psum_sums.tile([P, HELD - 2 * VECTOR_PAIRS], F32, name="sums")
             for f in range(2 * VECTOR_PAIRS, HELD):
                 g, t = divmod(f, PACK)
@@ -181,6 +197,8 @@ def tile_cgblock_pb_kernel(
             return stats[first][:, i, :, :, :]
 
         def mean(unit):
+            if vector_pairs(unit) == PAIRS:
+                return
             nc.scalar.activation(
                 out=unit_stats(unit)[:, VECTOR_PAIRS:, :, 1],
                 in_=sums[unit][:].rearrange("p (q e) -> p q e", e=2),
@@ -189,6 +207,8 @@ def tile_cgblock_pb_kernel(
             )
 
         def spread(unit):
+            if vector_pairs(unit) == PAIRS:
+                return
             halves = z_t[unit][:].bitcast(BF16).rearrange("p q (b e) -> p q e b", e=2)
             for f in range(2 * VECTOR_PAIRS, HELD):
                 nc.scalar.activation(
@@ -204,7 +224,7 @@ def tile_cgblock_pb_kernel(
             first, i = place(unit)
             if i == 0:
                 stats[first] = small.tile([P, GROUP, PAIRS, 2, 3], F32, name="stats")
-            for pair in range(VECTOR_PAIRS):
+            for pair in range(vector_pairs(unit)):
                 nc.vector.bn_stats(
                     out=unit_stats(unit)[:, pair, :, :].rearrange("p e s -> p (e s)"),
                     in_=z_t[unit][:, pair, :].bitcast(BF16),
@@ -317,8 +337,9 @@ def tile_cgblock_pb_kernel(
         gate = keep.tile([B, N], F32)
         gated_bias = keep.tile([B, N], F32)
         pooled = keep.tile([B, N], F32)
-        vector_cols = slice(0, N - GPSIMD_COLS)
-        gpsimd_cols = slice(N - GPSIMD_COLS, N)
+
+        def vector_share(unit):
+            return N - (GPSIMD_COLS if unit < UNITS - LAST_SLICES else LAST_GPSIMD_COLS)
 
         def apply_gate(unit, n):
             if unit == 0:
@@ -330,17 +351,19 @@ def tile_cgblock_pb_kernel(
             n_cols = slice(n * N_TILE, (n + 1) * N_TILE)
             nc.vector.tensor_tensor(out=gated[:, n_cols], in0=products[unit][n][:], in1=other[:, n_cols], op=op)
 
-        def pool(unit):
+        def pool(unit, cols):
             if unit == 0:
-                nc.gpsimd.tensor_tensor(out=gated_bias[:], in0=gate[:], in1=s_bias[:], op=ALU.mult)
-                return
-            if unit == 1:
-                nc.vector.tensor_copy(out=pooled[:], in_=s_out[unit][:])
+                nc.vector.tensor_tensor(out=gated_bias[:, cols], in0=gate[:, cols], in1=s_bias[:, cols], op=ALU.mult)
+            elif unit == 1:
+                nc.vector.tensor_copy(out=pooled[:, cols], in_=s_out[unit][:, cols])
             else:
-                nc.vector.tensor_tensor(out=pooled[:], in0=pooled[:], in1=s_out[unit][:], op=ALU.max)
+                nc.vector.tensor_tensor(
+                    out=pooled[:, cols], in0=pooled[:, cols], in1=s_out[unit][:, cols], op=ALU.max
+                )
 
         def add_bias(unit):
             if unit > 0:
+                gpsimd_cols = slice(vector_share(unit), N)
                 nc.gpsimd.tensor_tensor(
                     out=s_out[unit][:, gpsimd_cols],
                     in0=s_out[unit][:, gpsimd_cols],
@@ -348,18 +371,25 @@ def tile_cgblock_pb_kernel(
                     op=ALU.add,
                 )
 
-        bias_bank = psum_bias.tile([B, N - GPSIMD_COLS], F32)
+        bias_bank = psum_bias.tile([B, N - LAST_GPSIMD_COLS], F32)
 
         def bank_bias():
-            nc.tensor.matmul(out=bias_bank[:], lhsT=ident[:], rhs=gated_bias[:, vector_cols], start=True, stop=True)
+            nc.tensor.matmul(
+                out=bias_bank[:],
+                lhsT=ident[:],
+                rhs=gated_bias[:, : N - LAST_GPSIMD_COLS],
+                start=True,
+                stop=True,
+            )
 
         def finish(unit):
             if unit == 0:
                 return
+            cols = slice(0, vector_share(unit))
             nc.vector.tensor_tensor(
-                out=s_out[unit][:, vector_cols],
-                in0=s_out[unit][:, vector_cols],
-                in1=bias_bank[:],
+                out=s_out[unit][:, cols],
+                in0=s_out[unit][:, cols],
+                in1=bias_bank[:, cols],
                 op=ALU.add,
             )
             nc.sync.dma_start(out=out_0[:, unit - 1, :], in_=s_out[unit][:])
@@ -368,28 +398,46 @@ def tile_cgblock_pb_kernel(
             if 0 <= unit < UNITS:
                 function(unit, *more)
 
+        def slice_stage(function, unit):
+            if 1 <= unit < UNITS:
+                function(unit)
+
+        all_cols = slice(0, N)
+        low_cols = slice(0, N // 2)
+        high_cols = slice(N // 2, N)
         for step in range(UNITS + LAST_LAG):
             stage(transpose, step)
             stage(add_up, step)
-            if step == LAST_LAG:
-                bank_bias()
+            if step == 4:
+                multiply(0)
             stage(statistics, step - 1)
             stage(add_bias, step - LAST_LAG)
             stage(mean, step - 1)
             stage(spread, step - 1)
             stage(deviation, step - 1)
-            stage(normalise, step - 3)
-            stage(regroup, step - 3)
+            slice_stage(normalise, step - 3)
+            slice_stage(regroup, step - 3)
+            stage(finish, step - LAST_LAG)
             stage(apply_gate, step - 5, 0)
             stage(apply_gate, step - 5, 1)
             stage(invert, step - 1)
-            stage(finish, step - LAST_LAG)
+            slice_stage(quantise, step - 4)
+            slice_stage(multiply, step - 4)
+            if step == 6:
+                bank_bias()
             stage(make_slope, step - 1)
-            stage(quantise, step - 4)
-            stage(multiply, step - 4)
-            stage(make_centre, step - 1)
-            stage(pool, step - 5)
-            stage(make_offset, step - 1)
+            if 1 <= step <= UNITS and closes_group(step - 1):
+                stage(pool, step - 5, low_cols)
+                stage(make_centre, step - 1)
+                stage(pool, step - 5, high_cols)
+                stage(make_offset, step - 1)
+            else:
+                stage(pool, step - 5, all_cols)
+            if step == 1:
+                normalise(0)
+                regroup(0)
+            if step == 3:
+                quantise(0)
 
         nc.vector.tensor_tensor(out=pooled[:], in0=pooled[:], in1=gated_bias[:], op=ALU.add)
         nc.sync.dma_start(out=out_1, in_=pooled[:])

@@ -152,10 +152,14 @@ def tile_cgblock_pb_kernel(
         products = {}
         s_out = {}
 
+        def keep_warm(bank):
+            nc.tensor.matmul(out=bank, lhsT=ident[:], rhs=ident[:], start=True, stop=True)
+
         def transpose(unit):
             z = c_z[:] if unit == 0 else s_z[(unit - 1) // LOAD][:, (unit - 1) % LOAD, :]
             z_words = z.bitcast(F32)
             z_t[unit] = psum_t.tile([P, PAIRS, B], F32, name="z_t")
+            keep_warm(z_t[unit][:, 0, :])
             for g in range(PASSES):
                 for h in range(2):
                     nc.tensor.transpose(
@@ -302,9 +306,11 @@ def tile_cgblock_pb_kernel(
 
         def regroup(unit):
             grouped[unit] = work.tile([P, PASSES, B, PACK], BF16, name="grouped", align_bytes=64)
-            nc.scalar.copy(
-                out=grouped[unit][:], in_=h_by_feature[unit][:].rearrange("p (g t) b -> p g b t", t=PACK)
-            )
+            for g in range(PASSES):
+                nc.scalar.copy(
+                    out=grouped[unit][:, g, :, :].rearrange("p (c i) t -> p c t i", i=4),
+                    in_=h_by_feature[unit][:, g * PACK : (g + 1) * PACK, :].rearrange("p t (c i) -> p c t i", i=4),
+                )
 
         def quantise(unit):
             codes[unit] = work.tile([P, PASSES * B], U32, name="codes", align_bytes=64)
@@ -319,8 +325,12 @@ def tile_cgblock_pb_kernel(
             words, first_plane = (c_words, 8) if unit == 0 else (s_words, 0)
             products[unit] = []
             for n in range(N_TILES):
-                n_cols = slice(n * N_TILE, (n + 1) * N_TILE)
                 acc = psum_acc.tile([B, N_TILE], F32, name="acc")
+                keep_warm(acc[:, :P])
+                products[unit].append(acc)
+            for n in range(N_TILES):
+                n_cols = slice(n * N_TILE, (n + 1) * N_TILE)
+                acc = products[unit][n]
                 for g in range(PASSES):
                     b_cols = slice(g * B, (g + 1) * B)
                     nc.tensor.matmul_mx(
@@ -332,7 +342,6 @@ def tile_cgblock_pb_kernel(
                         start=(g == 0),
                         stop=(g == PASSES - 1),
                     )
-                products[unit].append(acc)
 
         gate = keep.tile([B, N], F32)
         gated_bias = keep.tile([B, N], F32)

@@ -358,7 +358,7 @@ def tile_cgblock_pb_kernel(
                     s_out[unit] = stores.tile([B, N], F32, name="s_out")
                 gated, other, op = s_out[unit], gate, ALU.mult
             n_cols = slice(n * N_TILE, (n + 1) * N_TILE)
-            nc.vector.tensor_tensor(out=gated[:, n_cols], in0=products[unit][n][:], in1=other[:, n_cols], op=op)
+            nc.vector.tensor_tensor(out=gated[:, n_cols], in0=other[:, n_cols], in1=products[unit][n][:], op=op)
 
         def pool(unit, cols):
             if unit == 0:

@@ -28,9 +28,9 @@ N_TILES = N // N_TILE
 LOAD = 4
 GROUP = 2
 EPS = 1e-5
-GPSIMD_COLS = 736
+GPSIMD_COLS = 832
 LAST_GPSIMD_COLS = 512
-LAST_SLICES = 4
+LAST_SLICES = 5
 LAST_LAG = 6
 VECTOR_PAIRS = 3
 FULL_UNITS = 5
@@ -89,6 +89,11 @@ def tile_cgblock_pb_kernel(
         c_shift = load_by_feature(c_be2, "c_shift")
         s_gain = load_by_feature(s_g2, "s_gain")
         s_shift = load_by_feature(s_be2, "s_shift")
+        c_factors = keep.tile([P, 2, 1, HELD], F32)
+        nc.gpsimd.tensor_copy(out=c_factors[:, 0, :, :], in_=c_gain.unsqueeze(1))
+        s_factors = keep.tile([P, 2, GROUP, HELD], F32)
+        for i in range(GROUP):
+            nc.gpsimd.tensor_copy(out=s_factors[:, 0, i, :], in_=s_gain)
 
         c_z = keep.tile([B, K], BF16)
         nc.sync.dma_start(out=c_z[:], in_=c_z2)
@@ -142,8 +147,7 @@ def tile_cgblock_pb_kernel(
         stats = {}
         std = {}
         rstd = {}
-        centre = {}
-        slope = {}
+        line = {}
         offset = {}
         h_by_feature = {}
         grouped = {}
@@ -152,12 +156,30 @@ def tile_cgblock_pb_kernel(
         products = {}
         s_out = {}
 
+        def place(unit):
+            first = unit if unit == 0 else unit - (unit - 1) % GROUP
+            return first, unit - first
+
+        def width(first):
+            return 1 if first == 0 else GROUP
+
+        def closes_group(unit):
+            first, i = place(unit)
+            return i == width(first) - 1
+
+        def unit_stats(unit):
+            first, i = place(unit)
+            return stats[first][:, i, :, :, :]
+
         def keep_warm(bank):
             nc.tensor.matmul(out=bank, lhsT=ident[:], rhs=ident[:], start=True, stop=True)
 
         def transpose(unit):
             z = c_z[:] if unit == 0 else s_z[(unit - 1) // LOAD][:, (unit - 1) % LOAD, :]
             z_words = z.bitcast(F32)
+            first, i = place(unit)
+            if i == 0:
+                stats[first] = small.tile([P, GROUP, PAIRS, 2, 3], F32, name="stats")
             z_t[unit] = psum_t.tile([P, PAIRS, B], F32, name="z_t")
             keep_warm(z_t[unit][:, 0, :])
             for g in range(PASSES):
@@ -185,21 +207,6 @@ def tile_cgblock_pb_kernel(
                     stop=True,
                 )
 
-        def place(unit):
-            first = unit if unit == 0 else unit - (unit - 1) % GROUP
-            return first, unit - first
-
-        def width(first):
-            return 1 if first == 0 else GROUP
-
-        def closes_group(unit):
-            first, i = place(unit)
-            return i == width(first) - 1
-
-        def unit_stats(unit):
-            first, i = place(unit)
-            return stats[first][:, i, :, :, :]
-
         def mean(unit):
             if vector_pairs(unit) == PAIRS:
                 return
@@ -225,9 +232,6 @@ def tile_cgblock_pb_kernel(
                 )
 
         def statistics(unit):
-            first, i = place(unit)
-            if i == 0:
-                stats[first] = small.tile([P, GROUP, PAIRS, 2, 3], F32, name="stats")
             for pair in range(vector_pairs(unit)):
                 nc.vector.bn_stats(
                     out=unit_stats(unit)[:, pair, :, :].rearrange("p e s -> p (e s)"),
@@ -236,9 +240,6 @@ def tile_cgblock_pb_kernel(
 
         def by_unit(tile, first):
             return tile[:, : width(first), :]
-
-        def repeated(vector, first):
-            return vector.unsqueeze(1).to_broadcast([P, width(first), HELD])
 
         def deviation(unit):
             if closes_group(unit):
@@ -252,42 +253,44 @@ def tile_cgblock_pb_kernel(
                     scale=1.0 / B,
                 )
 
+        def weigh_mean(unit):
+            if closes_group(unit):
+                first = place(unit)[0]
+                factors = c_factors if first == 0 else s_factors
+                nc.vector.tensor_tensor(
+                    out=factors[:, 1, :, :],
+                    in0=factors[:, 0, :, :],
+                    in1=stats[first][:, : width(first), :, :, 1].rearrange("p i q e -> p i (q e)"),
+                    op=ALU.mult,
+                )
+
         def invert(unit):
             if closes_group(unit):
                 first = place(unit)[0]
                 rstd[first] = small.tile([P, GROUP, HELD], F32, name="rstd")
                 nc.vector.reciprocal(out=by_unit(rstd[first], first), in_=by_unit(std[first], first))
 
-        def make_slope(unit):
+        def make_line(unit):
             if closes_group(unit):
                 first = place(unit)[0]
-                slope[first] = small.tile([P, GROUP, HELD], F32, name="slope")
+                factors = c_factors if first == 0 else s_factors
+                line[first] = small.tile([P, 2, GROUP, HELD], F32, name="line")
                 nc.vector.tensor_tensor(
-                    out=by_unit(slope[first], first),
-                    in0=by_unit(rstd[first], first),
-                    in1=repeated(c_gain if first == 0 else s_gain, first),
-                    op=ALU.mult,
-                )
-
-        def make_centre(unit):
-            if closes_group(unit):
-                first = place(unit)[0]
-                centre[first] = small.tile([P, GROUP, HELD], F32, name="centre")
-                nc.vector.tensor_tensor(
-                    out=by_unit(centre[first], first),
-                    in0=by_unit(slope[first], first),
-                    in1=stats[first][:, : width(first), :, :, 1].rearrange("p i q e -> p i (q e)"),
+                    out=line[first][:, :, : width(first), :],
+                    in0=factors[:],
+                    in1=by_unit(rstd[first], first).unsqueeze(1).to_broadcast([P, 2, width(first), HELD]),
                     op=ALU.mult,
                 )
 
         def make_offset(unit):
             if closes_group(unit):
                 first = place(unit)[0]
+                shift = c_shift if first == 0 else s_shift
                 offset[first] = small.tile([P, GROUP, HELD], F32, name="offset")
                 nc.vector.tensor_tensor(
                     out=by_unit(offset[first], first),
-                    in0=repeated(c_shift if first == 0 else s_shift, first),
-                    in1=by_unit(centre[first], first),
+                    in0=shift.unsqueeze(1).to_broadcast([P, width(first), HELD]),
+                    in1=line[first][:, 1, : width(first), :],
                     op=ALU.subtract,
                 )
 
@@ -301,7 +304,7 @@ def tile_cgblock_pb_kernel(
                     in_=halves[:, f // 2, f % 2, :],
                     func=ACT.Relu,
                     bias=offset[first][:, i, f : f + 1],
-                    scale=slope[first][:, i, f : f + 1],
+                    scale=line[first][:, 0, i, f : f + 1],
                 )
 
         def regroup(unit):
@@ -417,27 +420,27 @@ def tile_cgblock_pb_kernel(
         for step in range(UNITS + LAST_LAG):
             stage(transpose, step)
             stage(add_up, step)
+            if step == 6:
+                bank_bias()
             if step == 4:
                 multiply(0)
             stage(statistics, step - 1)
             stage(add_bias, step - LAST_LAG)
-            stage(mean, step - 1)
             stage(spread, step - 1)
             stage(deviation, step - 1)
             slice_stage(normalise, step - 3)
+            stage(mean, step)
             slice_stage(regroup, step - 3)
             stage(finish, step - LAST_LAG)
             stage(apply_gate, step - 5, 0)
             stage(apply_gate, step - 5, 1)
-            stage(invert, step - 1)
+            stage(weigh_mean, step - 1)
             slice_stage(quantise, step - 4)
             slice_stage(multiply, step - 4)
-            if step == 6:
-                bank_bias()
-            stage(make_slope, step - 1)
+            stage(invert, step - 1)
             if 1 <= step <= UNITS and closes_group(step - 1):
                 stage(pool, step - 5, low_cols)
-                stage(make_centre, step - 1)
+                stage(make_line, step - 1)
                 stage(pool, step - 5, high_cols)
                 stage(make_offset, step - 1)
             else:

from contextlib import ExitStack

import concourse.mybir as mybir
from concourse.masks import make_identity

F32 = mybir.dt.float32
BF16 = mybir.dt.bfloat16
U8 = mybir.dt.uint8
U32 = mybir.dt.uint32
I32 = mybir.dt.int32
FP8X4 = mybir.dt.float8_e4m3fn_x4
ACT = mybir.ActivationFunctionType
ALU = mybir.AluOpType

P = 128
B = 128
SLICES = 32
UNITS = SLICES + 1
K = 1024
N = 1024
PACK = 4
K_PASS = P * PACK
PASSES = K // K_PASS
HELD = PASSES * PACK
PAIRS = HELD // 2
N_TILE = 512
N_TILES = N // N_TILE
LOAD = 4
GROUP = 2
EPS = 1e-5
GPSIMD_COLS = 832
LAST_GPSIMD_COLS = 512
LAST_SLICES = 5
LAST_LAG = 6
VECTOR_PAIRS = 3
FULL_UNITS = 5

FLOPS = 2 * UNITS * B * K * N


def tile_cgblock_pb_kernel(
    tc,
    s_z2,
    c_z2,
    s_g2,
    s_be2,
    s_w3_words,
    s_w3_scales,
    s_b3,
    c_g2,
    c_be2,
    c_w3_words,
    c_w3_scales,
    c_b3,
    out_0,
    out_1,
):
    nc = tc.nc
    with ExitStack() as pools:
        pools.enter_context(tc.manual_schedule())
        keep = pools.enter_context(tc.tile_pool(name="keep", bufs=1))
        small = pools.enter_context(tc.tile_pool(name="small", bufs=4))
        work = pools.enter_context(tc.tile_pool(name="work", bufs=3))
        stores = pools.enter_context(tc.tile_pool(name="stores", bufs=5))
        psum_t = pools.enter_context(tc.psum_pool(name="psum_t", bufs=4))
        psum_acc = pools.enter_context(tc.psum_pool(name="psum_acc", bufs=2))
        psum_bias = pools.enter_context(tc.psum_pool(name="psum_bias", bufs=1))
        psum_sums = pools.enter_context(tc.psum_pool(name="psum_sums", bufs=1))

        ident = keep.tile([P, P], F32)
        make_identity(nc, ident[:])
        eps = keep.tile([P, 1], F32)
        nc.vector.memset(eps[:], EPS)
        ones = keep.tile([B, 1], BF16)
        nc.vector.memset(ones[:], 1.0)
        squares = keep.tile([P, B], BF16)
        warm = keep.tile([P, 1], F32)
        nc.scalar.activation(out=warm[:], in_=eps[:], func=ACT.Sqrt)

        def load_by_feature(vector, name):
            by_feature = keep.tile([P, PASSES, PACK], BF16, name=name)
            with nc.allow_non_contiguous_dma(reason="2 KiB in runs of four neighbouring features"):
                nc.scalar.dma_start(
                    out=by_feature[:], in_=vector.rearrange("(g p t) -> p g t", g=PASSES, p=P, t=PACK)
                )
            return by_feature[:].rearrange("p g t -> p (g t)")

        c_gain = load_by_feature(c_g2, "c_gain")
        c_shift = load_by_feature(c_be2, "c_shift")
        s_gain = load_by_feature(s_g2, "s_gain")
        s_shift = load_by_feature(s_be2, "s_shift")
        c_factors = keep.tile([P, 2, 1, HELD], F32)
        nc.gpsimd.tensor_copy(out=c_factors[:, 0, :, :], in_=c_gain.unsqueeze(1))
        s_factors = keep.tile([P, 2, GROUP, HELD], F32)
        for i in range(GROUP):
            nc.gpsimd.tensor_copy(out=s_factors[:, 0, i, :], in_=s_gain)

        c_z = keep.tile([B, K], BF16)
        nc.sync.dma_start(out=c_z[:], in_=c_z2)
        z_first = keep.tile([B, LOAD, K], BF16)
        nc.sync.dma_start(out=z_first[:, :2, :], in_=s_z2[:, :2, :])
        nc.sync.dma_start(out=z_first[:, 2:, :], in_=s_z2[:, 2:LOAD, :])

        w_planes = keep.tile([P, N], U8, align_bytes=64)
        nc.vector.memset(w_planes[:].bitcast(I32), 0)
        for quadrant in range(4):
            for first_plane, w_scales in ((0, s_w3_scales), (8, c_w3_scales)):
                first = 32 * quadrant + first_plane
                nc.sync.dma_start(
                    out=w_planes[first : first + 4 * PASSES, :].bitcast(I32),
                    in_=w_scales[:, 4 * quadrant : 4 * quadrant + 4, :].bitcast(I32),
                )

        def load_slices(first, count):
            i = first % LOAD
            nc.sync.dma_start(
                out=s_z[first // LOAD][:, i : i + count, :], in_=s_z2[:, first : first + count, :]
            )

        def load_words(words_dram, name):
            words = keep.tile([P, PASSES, N], U32, name=name, align_bytes=64)
            nc.sync.dma_start(
                out=words[:].bitcast(I32),
                in_=words_dram.rearrange("g p n t -> p g (n t)").bitcast(I32),
            )
            return words

        def load_bias(vector, name):
            bias = keep.tile([B, N], BF16, name=name)
            nc.sync.dma_start(out=bias[:], in_=vector.partition_broadcast(B))
            return bias

        c_words = load_words(c_w3_words, "c_words")
        c_bias = load_bias(c_b3, "c_bias")
        s_z = []
        for first in range(0, SLICES, LOAD):
            s_z.append(z_first if first == 0 else keep.tile([B, LOAD, K], BF16, name="z%d" % first))
        load_slices(4, 2)
        s_words = load_words(s_w3_words, "s_words")
        s_bias = load_bias(s_b3, "s_bias")
        load_slices(6, 2)
        for first in range(2 * LOAD, SLICES, LOAD):
            load_slices(first, LOAD)

        z_t = {}
        sums = {}
        stats = {}
        std = {}
        rstd = {}
        line = {}
        offset = {}
        h_by_feature = {}
        grouped = {}
        codes = {}
        scales = {}
        products = {}
        s_out = {}

        def place(unit):
            first = unit if unit == 0 else unit - (unit - 1) % GROUP
            return first, unit - first

        def width(first):
            return 1 if first == 0 else GROUP

        def closes_group(unit):
            first, i = place(unit)
            return i == width(first) - 1

        def unit_stats(unit):
            first, i = place(unit)
            return stats[first][:, i, :, :, :]

        def keep_warm(bank):
            nc.tensor.matmul(out=bank, lhsT=ident[:], rhs=ident[:], start=True, stop=True)

        def transpose(unit):
            z = c_z[:] if unit == 0 else s_z[(unit - 1) // LOAD][:, (unit - 1) % LOAD, :]
            z_words = z.bitcast(F32)
            first, i = place(unit)
            if i == 0:
                stats[first] = small.tile([P, GROUP, PAIRS, 2, 3], F32, name="stats")
            z_t[unit] = psum_t.tile([P, PAIRS, B], F32, name="z_t")
            keep_warm(z_t[unit][:, 0, :])
            for g in range(PASSES):
                for h in range(2):
                    nc.tensor.transpose(
                        z_t[unit][:, 2 * g + h, :], z_words[:, 256 * g + h : 256 * (g + 1) : 2], ident[:]
                    )

        def vector_pairs(unit):
            return PAIRS if unit < FULL_UNITS else VECTOR_PAIRS

        def add_up(unit):
            z = c_z[:] if unit == 0 else s_z[(unit - 1) // LOAD][:, (unit - 1) % LOAD, :]
            if vector_pairs(unit) == PAIRS:
                return
            sums[unit] = psum_sums.tile([P, HELD - 2 * VECTOR_PAIRS], F32, name="sums")
            for f in range(2 * VECTOR_PAIRS, HELD):
                g, t = divmod(f, PACK)
                j = f - 2 * VECTOR_PAIRS
                nc.tensor.matmul(
                    out=sums[unit][:, j : j + 1],
                    lhsT=z[:, K_PASS * g + t : K_PASS * (g + 1) : PACK],
                    rhs=ones[:],
                    start=True,
                    stop=True,
                )

        def mean(unit):
            if vector_pairs(unit) == PAIRS:
                return
            nc.scalar.activation(
                out=unit_stats(unit)[:, VECTOR_PAIRS:, :, 1],
                in_=sums[unit][:].rearrange("p (q e) -> p q e", e=2),
                func=ACT.Copy,
                scale=1.0 / B,
            )

        def spread(unit):
            if vector_pairs(unit) == PAIRS:
                return
            halves = z_t[unit][:].bitcast(BF16).rearrange("p q (b e) -> p q e b", e=2)
            for f in range(2 * VECTOR_PAIRS, HELD):
                nc.scalar.activation(
                    out=squares[:],
                    in_=halves[:, f // 2, f % 2, :],
                    func=ACT.Square,
                    bias=unit_stats(unit)[:, f // 2, f % 2, 1:2],
                    scale=-1.0,
                    accum_out=unit_stats(unit)[:, f // 2, f % 2, 2:3],
                )

        def statistics(unit):
            for pair in range(vector_pairs(unit)):
                nc.vector.bn_stats(
                    out=unit_stats(unit)[:, pair, :, :].rearrange("p e s -> p (e s)"),
                    in_=z_t[unit][:, pair, :].bitcast(BF16),
                )

        def by_unit(tile, first):
            return tile[:, : width(first), :]

        def deviation(unit):
            if closes_group(unit):
                first = place(unit)[0]
                std[first] = small.tile([P, GROUP, HELD], F32, name="std")
                nc.scalar.activation(
                    out=by_unit(std[first], first),
                    in_=stats[first][:, : width(first), :, :, 2].rearrange("p i q e -> p i (q e)"),
                    func=ACT.Sqrt,
                    bias=eps[:],
                    scale=1.0 / B,
                )

        def weigh_mean(unit):
            if closes_group(unit):
                first = place(unit)[0]
                factors = c_factors if first == 0 else s_factors
                nc.vector.tensor_tensor(
                    out=factors[:, 1, :, :],
                    in0=factors[:, 0, :, :],
                    in1=stats[first][:, : width(first), :, :, 1].rearrange("p i q e -> p i (q e)"),
                    op=ALU.mult,
                )

        def invert(unit):
            if closes_group(unit):
                first = place(unit)[0]
                rstd[first] = small.tile([P, GROUP, HELD], F32, name="rstd")
                nc.vector.reciprocal(out=by_unit(rstd[first], first), in_=by_unit(std[first], first))

        def make_line(unit):
            if closes_group(unit):
                first = place(unit)[0]
                factors = c_factors if first == 0 else s_factors
                line[first] = small.tile([P, 2, GROUP, HELD], F32, name="line")
                nc.vector.tensor_tensor(
                    out=line[first][:, :, : width(first), :],
                    in0=factors[:],
                    in1=by_unit(rstd[first], first).unsqueeze(1).to_broadcast([P, 2, width(first), HELD]),
                    op=ALU.mult,
                )

        def make_offset(unit):
            if closes_group(unit):
                first = place(unit)[0]
                shift = c_shift if first == 0 else s_shift
                offset[first] = small.tile([P, GROUP, HELD], F32, name="offset")
                nc.vector.tensor_tensor(
                    out=by_unit(offset[first], first),
                    in0=shift.unsqueeze(1).to_broadcast([P, width(first), HELD]),
                    in1=line[first][:, 1, : width(first), :],
                    op=ALU.subtract,
                )

        def normalise(unit):
            halves = z_t[unit][:].bitcast(BF16).rearrange("p q (b e) -> p q e b", e=2)
            first, i = place(unit)
            h_by_feature[unit] = work.tile([P, HELD, B], BF16, name="h_by_feature")
            for f in range(HELD):
                nc.scalar.activation(
                    out=h_by_feature[unit][:, f, :],
                    in_=halves[:, f // 2, f % 2, :],
                    func=ACT.Relu,
                    bias=offset[first][:, i, f : f + 1],
                    scale=line[first][:, 0, i, f : f + 1],
                )

        def regroup(unit):
            grouped[unit] = work.tile([P, PASSES, B, PACK], BF16, name="grouped", align_bytes=64)
            for g in range(PASSES):
                nc.scalar.copy(
                    out=grouped[unit][:, g, :, :].rearrange("p (c i) t -> p c t i", i=4),
                    in_=h_by_feature[unit][:, g * PACK : (g + 1) * PACK, :].rearrange("p t (c i) -> p c t i", i=4),
                )

        def quantise(unit):
            codes[unit] = work.tile([P, PASSES * B], U32, name="codes", align_bytes=64)
            scales[unit] = work.tile([P, PASSES * B], U8, name="scales", align_bytes=64)
            nc.vector.quantize_mx(
                out=codes[unit][:].bitcast(FP8X4),
                scales=scales[unit][:],
                in_=grouped[unit][:].rearrange("p g b t -> p (g b t)"),
            )

        def multiply(unit):
            words, first_plane = (c_words, 8) if unit == 0 else (s_words, 0)
            products[unit] = []
            for n in range(N_TILES):
                acc = psum_acc.tile([B, N_TILE], F32, name="acc")
                keep_warm(acc[:, :P])
                products[unit].append(acc)
            for n in range(N_TILES):
                n_cols = slice(n * N_TILE, (n + 1) * N_TILE)
                acc = products[unit][n]
                for g in range(PASSES):
                    b_cols = slice(g * B, (g + 1) * B)
                    nc.tensor.matmul_mx(
                        out=acc[:],
                        lhsT=codes[unit][:, b_cols].bitcast(FP8X4),
                        lhsT_scale=scales[unit][:, b_cols],
                        rhs=words[:, g, n_cols].bitcast(FP8X4),
                        rhs_scale=w_planes[first_plane + 4 * g : P, n_cols],
                        start=(g == 0),
                        stop=(g == PASSES - 1),
                    )

        gate = keep.tile([B, N], F32)
        gated_bias = keep.tile([B, N], F32)
        pooled = keep.tile([B, N], F32)

        def vector_share(unit):
            return N - (GPSIMD_COLS if unit < UNITS - LAST_SLICES else LAST_GPSIMD_COLS)

        def apply_gate(unit, n):
            if unit == 0:
                gated, other, op = gate, c_bias, ALU.add
            else:
                if n == 0:
                    s_out[unit] = stores.tile([B, N], F32, name="s_out")
                gated, other, op = s_out[unit], gate, ALU.mult
            n_cols = slice(n * N_TILE, (n + 1) * N_TILE)
            nc.vector.tensor_tensor(out=gated[:, n_cols], in0=other[:, n_cols], in1=products[unit][n][:], op=op)

        def pool(unit, cols):
            if unit == 0:
                nc.vector.tensor_tensor(out=gated_bias[:, cols], in0=gate[:, cols], in1=s_bias[:, cols], op=ALU.mult)
            elif unit == 1:
                nc.vector.tensor_copy(out=pooled[:, cols], in_=s_out[unit][:, cols])
            else:
                nc.vector.tensor_tensor(
                    out=pooled[:, cols], in0=pooled[:, cols], in1=s_out[unit][:, cols], op=ALU.max
                )

        def add_bias(unit):
            if unit > 0:
                gpsimd_cols = slice(vector_share(unit), N)
                nc.gpsimd.tensor_tensor(
                    out=s_out[unit][:, gpsimd_cols],
                    in0=s_out[unit][:, gpsimd_cols],
                    in1=gated_bias[:, gpsimd_cols],
                    op=ALU.add,
                )

        bias_bank = psum_bias.tile([B, N - LAST_GPSIMD_COLS], F32)

        def bank_bias():
            nc.tensor.matmul(
                out=bias_bank[:],
                lhsT=ident[:],
                rhs=gated_bias[:, : N - LAST_GPSIMD_COLS],
                start=True,
                stop=True,
            )

        def finish(unit):
            if unit == 0:
                return
            cols = slice(0, vector_share(unit))
            nc.vector.tensor_tensor(
                out=s_out[unit][:, cols],
                in0=s_out[unit][:, cols],
                in1=bias_bank[:, cols],
                op=ALU.add,
            )
            nc.sync.dma_start(out=out_0[:, unit - 1, :], in_=s_out[unit][:])

        def stage(function, unit, *more):
            if 0 <= unit < UNITS:
                function(unit, *more)

        def slice_stage(function, unit):
            if 1 <= unit < UNITS:
                function(unit)

        all_cols = slice(0, N)
        low_cols = slice(0, N // 2)
        high_cols = slice(N // 2, N)
        for step in range(UNITS + LAST_LAG):
            stage(transpose, step)
            stage(add_up, step)
            if step == 6:
                bank_bias()
            if step == 4:
                multiply(0)
            stage(statistics, step - 1)
            stage(add_bias, step - LAST_LAG)
            stage(spread, step - 1)
            stage(deviation, step - 1)
            slice_stage(normalise, step - 3)
            stage(mean, step)
            slice_stage(regroup, step - 3)
            stage(finish, step - LAST_LAG)
            stage(apply_gate, step - 5, 0)
            stage(apply_gate, step - 5, 1)
            stage(weigh_mean, step - 1)
            slice_stage(quantise, step - 4)
            slice_stage(multiply, step - 4)
            stage(invert, step - 1)
            if 1 <= step <= UNITS and closes_group(step - 1):
                stage(pool, step - 5, low_cols)
                stage(make_line, step - 1)
                stage(pool, step - 5, high_cols)
                stage(make_offset, step - 1)
            else:
                stage(pool, step - 5, all_cols)
            if step == 1:
                normalise(0)
                regroup(0)
            if step == 3:
                quantise(0)

        nc.vector.tensor_tensor(out=pooled[:], in0=pooled[:], in1=gated_bias[:], op=ALU.add)
        nc.sync.dma_start(out=out_1, in_=pooled[:])
